import numpy as np
import ml_dtypes


def mxq(x, axis, fmt="e4m3"):
    dtype, down = {"e4m3": (ml_dtypes.float8_e4m3fn, 7), "e5m2": (ml_dtypes.float8_e5m2, 14)}[fmt]
    v = np.moveaxis(np.asarray(x, np.float32).astype(ml_dtypes.bfloat16).astype(np.float64), axis, -1)
    blocks = v.reshape(v.shape[:-1] + (-1, 32))
    amax = np.abs(blocks).max(-1, keepdims=True)
    byte = np.maximum(np.where(amax > 0, np.frexp(amax)[1] - 1 + 127, 0) - down, 1)
    scale = np.exp2(byte - 127.0)
    codes = (blocks / scale).astype(np.float32).astype(dtype).astype(np.float64)
    return np.moveaxis((codes * scale).reshape(v.shape), -1, axis)


WIDE = False


def mx_kscale(k):
    if not WIDE:
        return np.ones(k)
    levels = np.array([10, -10, 5, -5, 0])
    a = np.random.permutation(np.resize(levels, k // 512 * 4)).reshape(k // 512, 4)
    idx = np.arange(k)
    return np.exp2(a[idx // 512, idx % 128 // 32])


BF16 = ml_dtypes.bfloat16


def bf(x):
    return np.asarray(x, np.float32).astype(BF16)


def f64(x):
    return np.asarray(x).astype(np.float64)


B, CLS, N, D = 8, 511, 512, 512
KEEP = 0.75
CEN = 0.75


def pm(shape):
    return np.where(np.random.random(shape) < 0.5, 1.0, -1.0)


def setup_inputs():
    s = mx_kscale(D)
    feat = CEN * pm((B, N, 1)) * pm((B, 1, D)) + np.random.standard_normal((B, N, D))
    return {"feat": bf(feat * s),
            "mask": bf(np.random.random((B, N)) < KEEP),
            "W": bf(np.random.standard_normal((D, D)) / np.sqrt(D) / s[:, None]),
            "b": bf(np.random.standard_normal((N, D)) * 0.2)}


def reference(feat, mask, W, b):
    x, m = f64(feat), f64(mask)
    nrm = np.sqrt(np.sum(x * x, axis=1, keepdims=True))
    xn = x / np.maximum(nrm, 1e-12) * m[:, :, None]
    xq = mxq(xn, 2, "e4m3")
    edge = xq @ xq.transpose(0, 2, 1)
    A = (np.maximum(edge, 0.0) + np.eye(N)[None]) * m[:, None, :]
    d = np.power(A.sum(-1) + 1e-8, -0.5)
    adj = d[:, :, None] * A * d[:, None, :]
    pre_sup = mxq(x, 2, "e4m3") @ mxq(f64(W), 0, "e4m3")
    out = np.tanh((mxq(adj, 2, "e4m3") @ mxq(pre_sup, 1, "e4m3")) + f64(b)[None]) * m[:, :, None]
    return out.transpose(0, 2, 1)

@@ -1,0 +1,331 @@
+from contextlib import ExitStack
+
+import concourse.mybir as mybir
+from concourse.masks import make_identity
+
+F32 = mybir.dt.float32
+BF16 = mybir.dt.bfloat16
+U32 = mybir.dt.uint32
+U8 = mybir.dt.uint8
+FP8X4 = mybir.dt.float8_e4m3fn_x4
+ALU = mybir.AluOpType
+ACT = mybir.ActivationFunctionType
+
+P = 128
+G = 8
+N = 512
+D = 512
+NT = N // P
+FLOPS = 3 * 2 * G * N * N * D
+
+
+def tile_graphlearner_pa_t_kernel(tc, feat, mask, W, b, out):
+    nc = tc.nc
+    with ExitStack() as ctx:
+        const = ctx.enter_context(tc.tile_pool(name="const", bufs=1))
+        work = ctx.enter_context(tc.tile_pool(name="work", bufs=3))
+        fin = ctx.enter_context(tc.tile_pool(name="fin", bufs=4))
+        stat = ctx.enter_context(tc.tile_pool(name="stat", bufs=3))
+        ptr = ctx.enter_context(tc.psum_pool(name="ptr", bufs=2))
+        pmm = ctx.enter_context(tc.psum_pool(name="pmm", bufs=4))
+        pdb = ctx.enter_context(tc.psum_pool(name="pdb", bufs=1))
+        pbt = ctx.enter_context(tc.psum_pool(name="pbt", bufs=1))
+        ctx.enter_context(tc.manual_schedule())
+
+        ident_f = const.tile([P, P], F32)
+        make_identity(nc, ident_f[:])
+        ident_b = const.tile([P, P], BF16)
+        make_identity(nc, ident_b[:])
+        neghalf = const.tile([P, NT], F32)
+        nc.vector.memset(neghalf[:], -0.5)
+        mrows = const.tile([P, P], BF16)
+        nc.vector.memset(mrows[:], 0.0)
+        nc.sync.dma_start(out=mrows[0 : G * NT, :], in_=mask.rearrange("g (i p) -> (g i) p", p=P))
+
+        f_sb = []
+        for g in range(G):
+            f_sb.append(const.tile([P, NT, D], BF16, name="f%d" % g))
+        wraw = const.tile([P, 4, D], BF16)
+        b_sb = const.tile([P, NT, D], BF16)
+
+        def load_feat(g):
+            nc.sync.dma_start(out=f_sb[g][:], in_=feat[g].rearrange("(i p) d -> p i d", p=P))
+
+        load_feat(0)
+        for u in range(2):
+            nc.sync.dma_start(
+                out=wraw[:, 2 * u : 2 * u + 2, :],
+                in_=W[256 * u : 256 * u + 256, :].rearrange("(q e) c -> q e c", e=2),
+            )
+        load_feat(1)
+        nc.sync.dma_start(out=b_sb[:], in_=b.rearrange("(i p) e -> p i e", p=P))
+        for g in range(2, G):
+            load_feat(g)
+
+        mT_ps = pbt.tile([P, P], BF16, tag="bt")
+        nc.tensor.transpose(mT_ps[:], mrows[:], ident_b[:])
+        maskT = const.tile([P, G * NT], F32)
+        nc.vector.tensor_copy(out=maskT[:], in_=mT_ps[:, 0 : G * NT])
+        maskeps = const.tile([P, G * NT], F32)
+        nc.vector.tensor_scalar_add(out=maskeps[:], in0=maskT[:], scalar1=1e-8)
+
+        dmf = const.tile([P, G * NT, P], F32)
+
+        def masked_identity(eng, g):
+            gs = slice(NT * g, NT * g + NT)
+            eng.tensor_tensor(
+                out=dmf[:, gs, :],
+                in0=ident_f[:].unsqueeze(1).to_broadcast([P, NT, P]),
+                in1=maskT[:, gs].unsqueeze(2).to_broadcast([P, NT, P]),
+                op=ALU.mult,
+            )
+
+        for g in range(G):
+            masked_identity(nc.vector if g < 3 else nc.gpsimd, g)
+
+        wg = const.tile([P, D * 4], BF16, align_bytes=64)
+        for u in range(2):
+            nc.vector.tensor_copy(
+                out=wg[:].rearrange("p (u e q t) -> p u e q t", u=2, e=2, t=4)[:, u],
+                in_=wraw[:].rearrange("p t (u q e) -> p u e q t", u=2, e=2)[:, u],
+            )
+        wcodes = const.tile([P, D], U32, align_bytes=64)
+        wscales = const.tile([P, D], U8, align_bytes=64)
+        nc.vector.quantize_mx(out=wcodes[:].bitcast(FP8X4), scales=wscales[:], in_=wg[:])
+
+        T = []
+        for g in range(G):
+            T.append({})
+
+        def words(g, i, u):
+            return f_sb[g][:, i, :].bitcast(F32)[:, P * u : P * u + P]
+
+        def st_trA(g):
+            for h in range(2):
+                ft = ptr.tile([P, 2, 256], F32, tag="tr")
+                T[g]["ft%d" % h] = ft
+                for u in range(2):
+                    for ii in range(2):
+                        nc.tensor.transpose(ft[:, u, P * ii : P * ii + P], words(g, 2 * h + ii, u), ident_f[:])
+
+        def fgc(g, h, copy):
+            if h == 0:
+                fg = work.tile([P, N * 4], BF16, align_bytes=64)
+                T[g]["fg"] = fg
+            fg32 = T[g]["fg"][:].bitcast(F32).rearrange("p (n u) -> p n u", u=2)
+            copy(out=fg32[:, 256 * h : 256 * h + 256, :], in_=T[g]["ft%d" % h][:].rearrange("p u n -> p n u"))
+
+        def st_sq(g):
+            ss = stat.tile([P, 4], F32)
+            T[g]["ss"] = ss
+            fg3 = T[g]["fg"][:].rearrange("p (n t) -> p n t", t=4)
+            for t in range(4):
+                junk = work.tile([P, N], BF16)
+                nc.scalar.activation(out=junk[:], in_=fg3[:, :, t], func=ACT.Square, accum_out=ss[:, t : t + 1])
+
+        def st_rn(g):
+            ssm = stat.tile([P, 4], F32)
+            nc.gpsimd.tensor_scalar_max(out=ssm[:], in0=T[g]["ss"][:], scalar1=1e-24)
+            rn = stat.tile([P, 4], F32)
+            T[g]["rn"] = rn
+            nc.gpsimd.tensor_tensor(out=rn[:], in0=ssm[:], in1=neghalf[:], op=ALU.pow)
+
+        def quantise(g, src, key):
+            codes = work.tile([P, N], U32, align_bytes=64, name=key + "c", tag=key + "c")
+            scales = work.tile([P, N], U8, align_bytes=64, name=key + "s", tag=key + "s")
+            T[g][key + "c"] = codes
+            T[g][key + "s"] = scales
+            nc.vector.quantize_mx(out=codes[:].bitcast(FP8X4), scales=scales[:], in_=T[g][src][:])
+
+        def mx(g, dst, lkey, lcols, rcodes, rscales):
+            nc.tensor.matmul_mx(
+                out=dst,
+                lhsT=T[g][lkey + "c"][:, lcols].bitcast(FP8X4),
+                lhsT_scale=T[g][lkey + "s"][:, lcols],
+                rhs=rcodes.bitcast(FP8X4),
+                rhs_scale=rscales,
+                start=True,
+                stop=True,
+            )
+
+        def st_trM(g):
+            for h in range(2):
+                fm = ptr.tile([P, 512], F32, tag="tr")
+                T[g]["fm%d" % h] = fm
+                for u in range(2):
+                    for ii in range(2):
+                        nc.tensor.transpose(
+                            fm[:, 256 * u + P * ii : 256 * u + P * ii + P],
+                            words(g, 2 * h + ii, u),
+                            dmf[:, NT * g + 2 * h + ii, :],
+                        )
+
+        def st_xg(g):
+            xg = work.tile([P, N * 4], BF16, align_bytes=64)
+            T[g]["xg"] = xg
+            xg4 = xg[:].rearrange("p (n u e) -> p n u e", u=2, e=2)
+            for h in range(2):
+                nc.vector.tensor_tensor(
+                    out=xg4[:, 256 * h : 256 * h + 256, :, :],
+                    in0=T[g]["fm%d" % h][:].bitcast(BF16).rearrange("p (u n e) -> p n u e", u=2, e=2),
+                    in1=T[g]["rn"][:].rearrange("p (u e) -> p u e", e=2).unsqueeze(1).to_broadcast([P, 256, 2, 2]),
+                    op=ALU.mult,
+                )
+
+        def st_psmm(g):
+            for j in range(4):
+                pj = pmm.tile([P, 4, P], F32, tag="mm")
+                T[g]["pj%d" % j] = pj
+                cols = slice(P * j, P * j + P)
+                for t in range(4):
+                    mx(g, pj[:, t, :], "f", slice(P * t, P * t + P), wcodes[:, cols], wscales[:, cols])
+
+        def pse(g, js, copy):
+            if js[0] == 0:
+                psg = work.tile([P, D * 4], BF16, align_bytes=64)
+                T[g]["psg"] = psg
+            psg3 = T[g]["psg"][:].rearrange("p (e t) -> p e t", t=4)
+            for j in js:
+                copy(out=psg3[:, P * j : P * j + P, :], in_=T[g]["pj%d" % j][:].rearrange("p t e -> p e t"))
+
+        def st_emm(g):
+            for t in range(4):
+                et = pmm.tile([P, N], F32, tag="mm")
+                T[g]["et%d" % t] = et
+                mx(g, et[:], "x", slice(P * t, P * t + P), T[g]["xc"][:], T[g]["xs"][:])
+
+        def st_relu(g):
+            r = work.tile([P, 5 * N], F32)
+            T[g]["r"] = r
+            deg = stat.tile([P, 4], F32)
+            T[g]["deg"] = deg
+            for t in range(4):
+                nc.scalar.activation(
+                    out=r[:, N * t : N * t + N], in_=T[g]["et%d" % t][:], func=ACT.Relu, accum_out=deg[:, t : t + 1]
+                )
+
+        def st_dch(g):
+            gs = slice(NT * g, NT * g + NT)
+            dg2 = stat.tile([P, 4], F32)
+            nc.gpsimd.tensor_tensor(out=dg2[:], in0=T[g]["deg"][:], in1=maskeps[:, gs], op=ALU.add)
+            dv = stat.tile([P, 4], F32)
+            T[g]["dv"] = dv
+            nc.gpsimd.tensor_tensor(out=dv[:], in0=dg2[:], in1=neghalf[:], op=ALU.pow)
+            dmk = stat.tile([P, 4], F32)
+            T[g]["dmk"] = dmk
+            nc.gpsimd.tensor_tensor(out=dmk[:], in0=dv[:], in1=maskT[:, gs], op=ALU.mult)
+
+        def st_diag(g):
+            rdiag = T[g]["r"][:].rearrange("p (t s) -> p t s", s=N + P)[:, :, 0:P]
+            nc.gpsimd.tensor_tensor(
+                out=rdiag, in0=rdiag, in1=ident_f[:].unsqueeze(1).to_broadcast([P, 4, P]), op=ALU.add
+            )
+
+        def st_scl(g):
+            r = T[g]["r"]
+            for t in range(4):
+                nc.gpsimd.tensor_scalar(
+                    out=r[:, N * t : N * t + N],
+                    in0=r[:, N * t : N * t + N],
+                    scalar1=T[g]["dmk"][:, t : t + 1],
+                    scalar2=0.0,
+                    op0=ALU.mult,
+                    op1=ALU.add,
+                )
+
+        def st_dbc(g):
+            dbc = pdb.tile([P, N], F32, tag="db")
+            T[g]["dbc"] = dbc
+            for i in range(NT):
+                nc.tensor.matmul(
+                    out=dbc[:, P * i : P * i + P],
+                    lhsT=T[g]["dv"][:, i : i + 1].to_broadcast([P, P]),
+                    rhs=ident_f[:],
+                    start=True,
+                    stop=True,
+                )
+
+        def st_p2(g):
+            adjg = work.tile([P, N * 4], BF16, align_bytes=64)
+            T[g]["ag"] = adjg
+            nc.vector.tensor_tensor(
+                out=adjg[:].rearrange("p (n t) -> p n t", t=4),
+                in0=T[g]["r"][:, 0 : 4 * N].rearrange("p (t n) -> p n t", t=4),
+                in1=T[g]["dbc"][:].unsqueeze(2).to_broadcast([P, N, 4]),
+                op=ALU.mult,
+            )
+
+        def bmt(g, u):
+            bt = pbt.tile([P, N], F32, tag="bt")
+            T[g]["bt%d" % u] = bt
+            for i in range(NT):
+                nc.tensor.transpose(
+                    bt[:, P * i : P * i + P],
+                    b_sb[:, i, :].bitcast(F32)[:, P * u : P * u + P],
+                    dmf[:, NT * g + i, :],
+                )
+
+        def bme(g, u, copy):
+            if u == 0:
+                bm = work.tile([P, 2, 2 * N], BF16)
+                T[g]["bm"] = bm
+            copy(out=T[g]["bm"][:, u, :].bitcast(F32), in_=T[g]["bt%d" % u][:])
+
+        def st_omm(g):
+            for j in range(4):
+                u, h = j // 2, j % 2
+                oj = pmm.tile([P, 2, 256], F32, tag="mm")
+                T[g]["oj%d" % j] = oj
+                cols = slice(256 * h, 256 * h + 256)
+                for e in range(2):
+                    mx(g, oj[:, e, :], "p", slice(P * (2 * u + e), P * (2 * u + e) + P), T[g]["ac"][:, cols], T[g]["as"][:, cols])
+
+        def st_z(g):
+            for j in range(4):
+                u, h = j // 2, j % 2
+                z = fin.tile([P, 2, 256], F32)
+                T[g]["z%d" % j] = z
+                bias = T[g]["bm"][:, u, :].rearrange("p (n e) -> p e n", e=2)[:, :, 256 * h : 256 * h + 256]
+                nc.vector.tensor_tensor(out=z[:], in0=T[g]["oj%d" % j][:], in1=bias, op=ALU.add)
+
+        def st_th(g):
+            rows = out[g].rearrange("(u q e) n -> u q e n", u=2, e=2)
+            for j in range(4):
+                u, h = j // 2, j % 2
+                y = fin.tile([P, 2, 256], F32)
+                nc.scalar.activation(out=y[:], in_=T[g]["z%d" % j][:], func=ACT.Tanh)
+                nc.sync.dma_start(out=rows[u][:, :, 256 * h : 256 * h + 256], in_=y[:])
+
+        def at(g, stage):
+            if 0 <= g < G:
+                stage(g)
+
+        for s in range(G + 3):
+            at(s - 2, lambda g: bme(g, 0, nc.scalar.copy))
+            at(s - 2, lambda g: st_dch(g))
+            at(s - 3, lambda g: st_th(g))
+            at(s - 1, lambda g: st_xg(g))
+            at(s - 1, lambda g: st_psmm(g))
+            at(s - 2, lambda g: bmt(g, 1))
+            at(s, lambda g: st_trA(g))
+            at(s - 2, lambda g: st_scl(g))
+            at(s, lambda g: fgc(g, 0, nc.vector.tensor_copy))
+            at(s - 1, lambda g: pse(g, (0, 1), nc.scalar.copy))
+            at(s - 1, lambda g: pse(g, (2, 3), nc.scalar.copy))
+            at(s, lambda g: fgc(g, 1, nc.scalar.copy))
+            at(s - 1, lambda g: quantise(g, "xg", "x"))
+            at(s - 2, lambda g: bme(g, 1, nc.vector.tensor_copy))
+            at(s - 2, lambda g: st_dbc(g))
+            at(s - 1, lambda g: quantise(g, "psg", "p"))
+            at(s - 1, lambda g: st_emm(g))
+            at(s, lambda g: st_sq(g))
+            at(s - 2, lambda g: st_p2(g))
+            at(s - 2, lambda g: quantise(g, "ag", "a"))
+            at(s, lambda g: quantise(g, "fg", "f"))
+            at(s - 1, lambda g: bmt(g, 0))
+            at(s - 1, lambda g: st_relu(g))
+            at(s - 2, lambda g: st_omm(g))
+            at(s, lambda g: st_rn(g))
+            at(s, lambda g: st_trM(g))
+            at(s - 1, lambda g: st_diag(g))
+            at(s - 2, lambda g: st_z(g))

@@ -16,21 +16,34 @@ G = 8
 N = 512
 D = 512
 NT = N // P
+HALF = N // 2
 FLOPS = 3 * 2 * G * N * N * D
 
 
 def tile_graphlearner_pa_t_kernel(tc, feat, mask, W, b, out):
     nc = tc.nc
+
+    def at(g, stage):
+        if 0 <= g < G:
+            stage(g)
+
+    def quantise(codes, scales, grouped):
+        nc.vector.quantize_mx(out=codes[:].bitcast(FP8X4), scales=scales[:], in_=grouped[:])
+
+    def mx(dst, lcodes, lscales, rcodes, rscales):
+        nc.tensor.matmul_mx(
+            out=dst,
+            lhsT=lcodes.bitcast(FP8X4),
+            lhsT_scale=lscales,
+            rhs=rcodes.bitcast(FP8X4),
+            rhs_scale=rscales,
+            start=True,
+            stop=True,
+        )
+
     with ExitStack() as ctx:
-        const = ctx.enter_context(tc.tile_pool(name="const", bufs=1))
-        work = ctx.enter_context(tc.tile_pool(name="work", bufs=3))
-        fin = ctx.enter_context(tc.tile_pool(name="fin", bufs=4))
-        stat = ctx.enter_context(tc.tile_pool(name="stat", bufs=3))
-        ptr = ctx.enter_context(tc.psum_pool(name="ptr", bufs=2))
-        pmm = ctx.enter_context(tc.psum_pool(name="pmm", bufs=4))
-        pdb = ctx.enter_context(tc.psum_pool(name="pdb", bufs=1))
-        pbt = ctx.enter_context(tc.psum_pool(name="pbt", bufs=1))
         ctx.enter_context(tc.manual_schedule())
+        const = ctx.enter_context(tc.tile_pool(name="const", bufs=1))
 
         ident_f = const.tile([P, P], F32)
         make_identity(nc, ident_f[:])
@@ -40,292 +53,330 @@ def tile_graphlearner_pa_t_kernel(tc, feat, mask, W, b, out):
         nc.vector.memset(neghalf[:], -0.5)
         mrows = const.tile([P, P], BF16)
         nc.vector.memset(mrows[:], 0.0)
-        nc.sync.dma_start(out=mrows[0 : G * NT, :], in_=mask.rearrange("g (i p) -> (g i) p", p=P))
-
-        f_sb = []
-        for g in range(G):
-            f_sb.append(const.tile([P, NT, D], BF16, name="f%d" % g))
-        wraw = const.tile([P, 4, D], BF16)
-        b_sb = const.tile([P, NT, D], BF16)
-
-        def load_feat(g):
-            nc.sync.dma_start(out=f_sb[g][:], in_=feat[g].rearrange("(i p) d -> p i d", p=P))
-
-        load_feat(0)
-        for u in range(2):
-            nc.sync.dma_start(
-                out=wraw[:, 2 * u : 2 * u + 2, :],
-                in_=W[256 * u : 256 * u + 256, :].rearrange("(q e) c -> q e c", e=2),
-            )
-        load_feat(1)
-        nc.sync.dma_start(out=b_sb[:], in_=b.rearrange("(i p) e -> p i e", p=P))
-        for g in range(2, G):
-            load_feat(g)
-
-        mT_ps = pbt.tile([P, P], BF16, tag="bt")
-        nc.tensor.transpose(mT_ps[:], mrows[:], ident_b[:])
         maskT = const.tile([P, G * NT], F32)
-        nc.vector.tensor_copy(out=maskT[:], in_=mT_ps[:, 0 : G * NT])
         maskeps = const.tile([P, G * NT], F32)
-        nc.vector.tensor_scalar_add(out=maskeps[:], in0=maskT[:], scalar1=1e-8)
-
         dmf = const.tile([P, G * NT, P], F32)
-
-        def masked_identity(eng, g):
-            gs = slice(NT * g, NT * g + NT)
-            eng.tensor_tensor(
-                out=dmf[:, gs, :],
-                in0=ident_f[:].unsqueeze(1).to_broadcast([P, NT, P]),
-                in1=maskT[:, gs].unsqueeze(2).to_broadcast([P, NT, P]),
-                op=ALU.mult,
-            )
-
-        for g in range(G):
-            masked_identity(nc.vector if g < 3 else nc.gpsimd, g)
-
-        wg = const.tile([P, D * 4], BF16, align_bytes=64)
-        for u in range(2):
-            nc.vector.tensor_copy(
-                out=wg[:].rearrange("p (u e q t) -> p u e q t", u=2, e=2, t=4)[:, u],
-                in_=wraw[:].rearrange("p t (u q e) -> p u e q t", u=2, e=2)[:, u],
-            )
+        b_sb = const.tile([P, NT, D], BF16)
         wcodes = const.tile([P, D], U32, align_bytes=64)
         wscales = const.tile([P, D], U8, align_bytes=64)
-        nc.vector.quantize_mx(out=wcodes[:].bitcast(FP8X4), scales=wscales[:], in_=wg[:])
-
+        deg = const.tile([P, G, 2, 8], F32)
+        fcodes = []
+        fscales = []
+        r = []
+        for g in range(G):
+            fcodes.append(const.tile([P, N], U32, align_bytes=64, name="fc%d" % g))
+            fscales.append(const.tile([P, N], U8, align_bytes=64, name="fs%d" % g))
+            r.append(const.tile([P, 5 * N], F32, name="r%d" % g))
         T = []
         for g in range(G):
             T.append({})
 
-        def words(g, i, u):
-            return f_sb[g][:, i, :].bitcast(F32)[:, P * u : P * u + P]
+        with ExitStack() as one:
+            big = one.enter_context(tc.tile_pool(name="big", bufs=1))
+            work = one.enter_context(tc.tile_pool(name="work", bufs=3))
+            ptr = one.enter_context(tc.psum_pool(name="ptr", bufs=4))
+            pmm = one.enter_context(tc.psum_pool(name="pmm", bufs=4))
 
-        def st_trA(g):
-            for h in range(2):
-                ft = ptr.tile([P, 2, 256], F32, tag="tr")
-                T[g]["ft%d" % h] = ft
-                for u in range(2):
-                    for ii in range(2):
-                        nc.tensor.transpose(ft[:, u, P * ii : P * ii + P], words(g, 2 * h + ii, u), ident_f[:])
+            f_sb = []
+            for g in range(G):
+                f_sb.append(big.tile([P, NT, D], BF16, name="f%d" % g))
+            wraw = big.tile([P, 4, D], BF16)
+            wg = big.tile([P, D * 4], BF16, align_bytes=64)
 
-        def fgc(g, h, copy):
-            if h == 0:
-                fg = work.tile([P, N * 4], BF16, align_bytes=64)
-                T[g]["fg"] = fg
-            fg32 = T[g]["fg"][:].bitcast(F32).rearrange("p (n u) -> p n u", u=2)
-            copy(out=fg32[:, 256 * h : 256 * h + 256, :], in_=T[g]["ft%d" % h][:].rearrange("p u n -> p n u"))
+            nc.sync.dma_start(out=mrows[0 : G * NT, :], in_=mask.rearrange("g (i p) -> (g i) p", p=P))
+            nc.sync.dma_start(out=f_sb[0][:], in_=feat[0].rearrange("(i p) d -> p i d", p=P))
+            for u in range(2):
+                nc.sync.dma_start(
+                    out=wraw[:, 2 * u : 2 * u + 2, :],
+                    in_=W[256 * u : 256 * u + 256, :].rearrange("(q e) c -> q e c", e=2),
+                )
+            for g in range(1, G):
+                nc.sync.dma_start(out=f_sb[g][:], in_=feat[g].rearrange("(i p) d -> p i d", p=P))
+            nc.sync.dma_start(out=b_sb[:], in_=b.rearrange("(i p) e -> p i e", p=P))
 
-        def st_sq(g):
-            ss = stat.tile([P, 4], F32)
-            T[g]["ss"] = ss
-            fg3 = T[g]["fg"][:].rearrange("p (n t) -> p n t", t=4)
-            for t in range(4):
-                junk = work.tile([P, N], BF16)
-                nc.scalar.activation(out=junk[:], in_=fg3[:, :, t], func=ACT.Square, accum_out=ss[:, t : t + 1])
+            mT_ps = ptr.tile([P, P], BF16, tag="tr")
+            nc.tensor.transpose(mT_ps[:], mrows[:], ident_b[:])
+            nc.vector.tensor_copy(out=maskT[:], in_=mT_ps[:, 0 : G * NT])
+            nc.vector.tensor_scalar_add(out=maskeps[:], in0=maskT[:], scalar1=1e-8)
 
-        def st_rn(g):
-            ssm = stat.tile([P, 4], F32)
-            nc.gpsimd.tensor_scalar_max(out=ssm[:], in0=T[g]["ss"][:], scalar1=1e-24)
-            rn = stat.tile([P, 4], F32)
-            T[g]["rn"] = rn
-            nc.gpsimd.tensor_tensor(out=rn[:], in0=ssm[:], in1=neghalf[:], op=ALU.pow)
-
-        def quantise(g, src, key):
-            codes = work.tile([P, N], U32, align_bytes=64, name=key + "c", tag=key + "c")
-            scales = work.tile([P, N], U8, align_bytes=64, name=key + "s", tag=key + "s")
-            T[g][key + "c"] = codes
-            T[g][key + "s"] = scales
-            nc.vector.quantize_mx(out=codes[:].bitcast(FP8X4), scales=scales[:], in_=T[g][src][:])
-
-        def mx(g, dst, lkey, lcols, rcodes, rscales):
-            nc.tensor.matmul_mx(
-                out=dst,
-                lhsT=T[g][lkey + "c"][:, lcols].bitcast(FP8X4),
-                lhsT_scale=T[g][lkey + "s"][:, lcols],
-                rhs=rcodes.bitcast(FP8X4),
-                rhs_scale=rscales,
-                start=True,
-                stop=True,
-            )
-
-        def st_trM(g):
-            for h in range(2):
-                fm = ptr.tile([P, 512], F32, tag="tr")
-                T[g]["fm%d" % h] = fm
-                for u in range(2):
-                    for ii in range(2):
-                        nc.tensor.transpose(
-                            fm[:, 256 * u + P * ii : 256 * u + P * ii + P],
-                            words(g, 2 * h + ii, u),
-                            dmf[:, NT * g + 2 * h + ii, :],
-                        )
-
-        def st_xg(g):
-            xg = work.tile([P, N * 4], BF16, align_bytes=64)
-            T[g]["xg"] = xg
-            xg4 = xg[:].rearrange("p (n u e) -> p n u e", u=2, e=2)
-            for h in range(2):
+            def masked_identity(g):
+                gs = slice(NT * g, NT * g + NT)
                 nc.vector.tensor_tensor(
-                    out=xg4[:, 256 * h : 256 * h + 256, :, :],
-                    in0=T[g]["fm%d" % h][:].bitcast(BF16).rearrange("p (u n e) -> p n u e", u=2, e=2),
-                    in1=T[g]["rn"][:].rearrange("p (u e) -> p u e", e=2).unsqueeze(1).to_broadcast([P, 256, 2, 2]),
+                    out=dmf[:, gs, :],
+                    in0=ident_f[:].unsqueeze(1).to_broadcast([P, NT, P]),
+                    in1=maskT[:, gs].unsqueeze(2).to_broadcast([P, NT, P]),
                     op=ALU.mult,
                 )
 
-        def st_psmm(g):
-            for j in range(4):
-                pj = pmm.tile([P, 4, P], F32, tag="mm")
-                T[g]["pj%d" % j] = pj
-                cols = slice(P * j, P * j + P)
-                for t in range(4):
-                    mx(g, pj[:, t, :], "f", slice(P * t, P * t + P), wcodes[:, cols], wscales[:, cols])
+            def quantise_w(g):
+                for u in range(2):
+                    nc.vector.tensor_copy(
+                        out=wg[:].rearrange("p (u e q t) -> p u e q t", u=2, e=2, t=4)[:, u],
+                        in_=wraw[:].rearrange("p t (u q e) -> p u e q t", u=2, e=2)[:, u],
+                    )
+                quantise(wcodes, wscales, wg)
 
-        def pse(g, js, copy):
-            if js[0] == 0:
+            def words(g, i, u):
+                return f_sb[g][:, i, :].bitcast(F32)[:, P * u : P * u + P]
+
+            def transposes(g, key, identity_of):
+                for h in range(2):
+                    ft = ptr.tile([P, 2, HALF], F32, tag="tr")
+                    T[g][key + str(h)] = ft
+                    for u in range(2):
+                        for ii in range(2):
+                            nc.tensor.transpose(
+                                ft[:, u, P * ii : P * ii + P], words(g, 2 * h + ii, u), identity_of(2 * h + ii)
+                            )
+
+            def plain_transposes(g):
+                transposes(g, "ft", lambda i: ident_f[:])
+
+            def masked_transposes(g):
+                transposes(g, "fm", lambda i: dmf[:, NT * g + i, :])
+
+            def copy_features(g):
+                fg = work.tile([P, N * 4], BF16, align_bytes=64)
+                T[g]["fg"] = fg
+                fg32 = fg[:].bitcast(F32).rearrange("p (n u) -> p n u", u=2)
+                for h in range(2):
+                    nc.scalar.copy(
+                        out=fg32[:, HALF * h : HALF * h + HALF, :], in_=T[g]["ft" + str(h)][:].rearrange("p u n -> p n u")
+                    )
+
+            def squares(g):
+                ss = work.tile([P, 4], F32)
+                T[g]["ss"] = ss
+                fg3 = T[g]["fg"][:].rearrange("p (n t) -> p n t", t=4)
+                for t in range(4):
+                    junk = work.tile([P, N], BF16)
+                    nc.scalar.activation(out=junk[:], in_=fg3[:, :, t], func=ACT.Square, accum_out=ss[:, t : t + 1])
+
+            def inverse_norms(g):
+                ssm = work.tile([P, 4], F32)
+                nc.gpsimd.tensor_scalar_max(out=ssm[:], in0=T[g]["ss"][:], scalar1=1e-24)
+                rn = work.tile([P, 4], F32)
+                T[g]["rn"] = rn
+                nc.gpsimd.tensor_tensor(out=rn[:], in0=ssm[:], in1=neghalf[:], op=ALU.pow)
+
+            def quantise_features(g):
+                quantise(fcodes[g], fscales[g], T[g]["fg"])
+
+            def normed_features(g):
+                xg = work.tile([P, N * 4], BF16, align_bytes=64)
+                T[g]["xg"] = xg
+                xg4 = xg[:].rearrange("p (n u e) -> p n u e", u=2, e=2)
+                for h in range(2):
+                    nc.vector.tensor_tensor(
+                        out=xg4[:, HALF * h : HALF * h + HALF, :, :],
+                        in0=T[g]["fm" + str(h)][:]
+                        .rearrange("p u n -> p (u n)")
+                        .bitcast(BF16)
+                        .rearrange("p (u n e) -> p n u e", u=2, e=2),
+                        in1=T[g]["rn"][:].rearrange("p (u e) -> p u e", e=2).unsqueeze(1).to_broadcast([P, HALF, 2, 2]),
+                        op=ALU.mult,
+                    )
+
+            def quantise_normed(g):
+                xc = work.tile([P, N], U32, align_bytes=64)
+                xs = work.tile([P, N], U8, align_bytes=64)
+                T[g]["xc"] = xc
+                T[g]["xs"] = xs
+                quantise(xc, xs, T[g]["xg"])
+
+            def edge(g):
+                for t in range(4):
+                    et = pmm.tile([P, N], F32, tag="mm")
+                    T[g]["et" + str(t)] = et
+                    cols = slice(P * t, P * t + P)
+                    mx(et[:], T[g]["xc"][:, cols], T[g]["xs"][:, cols], T[g]["xc"][:], T[g]["xs"][:])
+
+            def relu_scalar(g):
+                for t in range(2):
+                    nc.scalar.activation(
+                        out=r[g][:, N * t : N * t + N],
+                        in_=T[g]["et" + str(t)][:],
+                        func=ACT.Relu,
+                        accum_out=deg[:, g, 0, t : t + 1],
+                    )
+
+            def relu_vector(g):
+                for t in range(2, 4):
+                    nc.vector.tensor_scalar(
+                        out=r[g][:, N * t : N * t + N],
+                        in0=T[g]["et" + str(t)][:],
+                        scalar1=0.0,
+                        scalar2=None,
+                        op0=ALU.max,
+                        op1=ALU.add,
+                        accum_out=deg[:, g, 1, t - 2 : t - 1],
+                    )
+
+            for s in range(-3, G + 3):
+                at(s, copy_features)
+                at(s - 3, relu_scalar)
+                at(s, squares)
+                at(s - 1, masked_transposes)
+                at(s - 2, quantise_normed)
+                at(s + 1, plain_transposes)
+                at(s - 3, relu_vector)
+                at(s + 3, masked_identity)
+                at(s, quantise_features)
+                if s == 0:
+                    quantise_w(s)
+                at(s - 1, normed_features)
+                at(s, inverse_norms)
+                at(s - 2, edge)
+
+        with ExitStack() as two:
+            work = two.enter_context(tc.tile_pool(name="work2", bufs=2))
+            small = two.enter_context(tc.tile_pool(name="small", bufs=4))
+            bias_pool = two.enter_context(tc.tile_pool(name="bias", bufs=3))
+            zpool = two.enter_context(tc.tile_pool(name="zpool", bufs=8))
+            ypool = two.enter_context(tc.tile_pool(name="ypool", bufs=4))
+            pmm = two.enter_context(tc.psum_pool(name="pmm2", bufs=5))
+            pbt = two.enter_context(tc.psum_pool(name="pbt", bufs=2))
+            pdb = two.enter_context(tc.psum_pool(name="pdb", bufs=1))
+
+            def add_identity(g):
+                rdiag = r[g][:].rearrange("p (t s) -> p t s", s=N + P)[:, :, 0:P]
+                nc.gpsimd.tensor_tensor(
+                    out=rdiag, in0=rdiag, in1=ident_f[:].unsqueeze(1).to_broadcast([P, 4, P]), op=ALU.add
+                )
+
+            def inverse_root_degrees(g):
+                gs = slice(NT * g, NT * g + NT)
+                dg2 = small.tile([P, 2, 2], F32)
+                nc.gpsimd.tensor_tensor(
+                    out=dg2[:],
+                    in0=deg[:, g, :, 0:2],
+                    in1=maskeps[:, gs].rearrange("p (a c) -> p a c", c=2),
+                    op=ALU.add,
+                )
+                dv = small.tile([P, 4], F32)
+                T[g]["dv"] = dv
+                nc.gpsimd.tensor_tensor(
+                    out=dv[:], in0=dg2[:].rearrange("p a c -> p (a c)"), in1=neghalf[:], op=ALU.pow
+                )
+
+            def scale_rows(g):
+                for t in range(4):
+                    nc.gpsimd.tensor_scalar(
+                        out=r[g][:, N * t : N * t + N],
+                        in0=r[g][:, N * t : N * t + N],
+                        scalar1=T[g]["dv"][:, t : t + 1],
+                        scalar2=maskT[:, NT * g + t : NT * g + t + 1],
+                        op0=ALU.mult,
+                        op1=ALU.mult,
+                    )
+
+            def spread_d(g):
+                dbc = pdb.tile([P, N], F32, tag="db")
+                T[g]["dbc"] = dbc
+                for i in range(NT):
+                    nc.tensor.matmul(
+                        out=dbc[:, P * i : P * i + P],
+                        lhsT=T[g]["dv"][:, i : i + 1].to_broadcast([P, P]),
+                        rhs=ident_f[:],
+                        start=True,
+                        stop=True,
+                    )
+
+            def pre_sup(g):
+                for j in range(4):
+                    pj = pmm.tile([P, 4, P], F32, tag="mm")
+                    T[g]["pj" + str(j)] = pj
+                    cols = slice(P * j, P * j + P)
+                    for t in range(4):
+                        rows = slice(P * t, P * t + P)
+                        mx(pj[:, t, :], fcodes[g][:, rows], fscales[g][:, rows], wcodes[:, cols], wscales[:, cols])
+
+            def copy_pre_sup(g):
                 psg = work.tile([P, D * 4], BF16, align_bytes=64)
                 T[g]["psg"] = psg
-            psg3 = T[g]["psg"][:].rearrange("p (e t) -> p e t", t=4)
-            for j in js:
-                copy(out=psg3[:, P * j : P * j + P, :], in_=T[g]["pj%d" % j][:].rearrange("p t e -> p e t"))
+                psg3 = psg[:].rearrange("p (e t) -> p e t", t=4)
+                for j in range(4):
+                    nc.scalar.copy(out=psg3[:, P * j : P * j + P, :], in_=T[g]["pj" + str(j)][:].rearrange("p t e -> p e t"))
 
-        def st_emm(g):
-            for t in range(4):
-                et = pmm.tile([P, N], F32, tag="mm")
-                T[g]["et%d" % t] = et
-                mx(g, et[:], "x", slice(P * t, P * t + P), T[g]["xc"][:], T[g]["xs"][:])
+            def quantise_pre_sup(g):
+                pc = work.tile([P, D], U32, align_bytes=64)
+                ps = work.tile([P, D], U8, align_bytes=64)
+                T[g]["pc"] = pc
+                T[g]["ps"] = ps
+                quantise(pc, ps, T[g]["psg"])
 
-        def st_relu(g):
-            r = work.tile([P, 5 * N], F32)
-            T[g]["r"] = r
-            deg = stat.tile([P, 4], F32)
-            T[g]["deg"] = deg
-            for t in range(4):
-                nc.scalar.activation(
-                    out=r[:, N * t : N * t + N], in_=T[g]["et%d" % t][:], func=ACT.Relu, accum_out=deg[:, t : t + 1]
+            def scale_columns(g):
+                adjg = work.tile([P, N * 4], BF16, align_bytes=64)
+                T[g]["ag"] = adjg
+                nc.vector.tensor_tensor(
+                    out=adjg[:].rearrange("p (n t) -> p n t", t=4),
+                    in0=r[g][:, 0 : 4 * N].rearrange("p (t n) -> p n t", t=4),
+                    in1=T[g]["dbc"][:].unsqueeze(2).to_broadcast([P, N, 4]),
+                    op=ALU.mult,
                 )
 
-        def st_dch(g):
-            gs = slice(NT * g, NT * g + NT)
-            dg2 = stat.tile([P, 4], F32)
-            nc.gpsimd.tensor_tensor(out=dg2[:], in0=T[g]["deg"][:], in1=maskeps[:, gs], op=ALU.add)
-            dv = stat.tile([P, 4], F32)
-            T[g]["dv"] = dv
-            nc.gpsimd.tensor_tensor(out=dv[:], in0=dg2[:], in1=neghalf[:], op=ALU.pow)
-            dmk = stat.tile([P, 4], F32)
-            T[g]["dmk"] = dmk
-            nc.gpsimd.tensor_tensor(out=dmk[:], in0=dv[:], in1=maskT[:, gs], op=ALU.mult)
+            def quantise_adj(g):
+                ac = work.tile([P, N], U32, align_bytes=64)
+                asc = work.tile([P, N], U8, align_bytes=64)
+                T[g]["ac"] = ac
+                T[g]["as"] = asc
+                quantise(ac, asc, T[g]["ag"])
 
-        def st_diag(g):
-            rdiag = T[g]["r"][:].rearrange("p (t s) -> p t s", s=N + P)[:, :, 0:P]
-            nc.gpsimd.tensor_tensor(
-                out=rdiag, in0=rdiag, in1=ident_f[:].unsqueeze(1).to_broadcast([P, 4, P]), op=ALU.add
-            )
+            def bias_transposes(g):
+                for u in range(2):
+                    bt = pbt.tile([P, N], F32, tag="bt")
+                    T[g]["bt" + str(u)] = bt
+                    for i in range(NT):
+                        nc.tensor.transpose(
+                            bt[:, P * i : P * i + P],
+                            b_sb[:, i, :].bitcast(F32)[:, P * u : P * u + P],
+                            dmf[:, NT * g + i, :],
+                        )
 
-        def st_scl(g):
-            r = T[g]["r"]
-            for t in range(4):
-                nc.gpsimd.tensor_scalar(
-                    out=r[:, N * t : N * t + N],
-                    in0=r[:, N * t : N * t + N],
-                    scalar1=T[g]["dmk"][:, t : t + 1],
-                    scalar2=0.0,
-                    op0=ALU.mult,
-                    op1=ALU.add,
-                )
-
-        def st_dbc(g):
-            dbc = pdb.tile([P, N], F32, tag="db")
-            T[g]["dbc"] = dbc
-            for i in range(NT):
-                nc.tensor.matmul(
-                    out=dbc[:, P * i : P * i + P],
-                    lhsT=T[g]["dv"][:, i : i + 1].to_broadcast([P, P]),
-                    rhs=ident_f[:],
-                    start=True,
-                    stop=True,
-                )
-
-        def st_p2(g):
-            adjg = work.tile([P, N * 4], BF16, align_bytes=64)
-            T[g]["ag"] = adjg
-            nc.vector.tensor_tensor(
-                out=adjg[:].rearrange("p (n t) -> p n t", t=4),
-                in0=T[g]["r"][:, 0 : 4 * N].rearrange("p (t n) -> p n t", t=4),
-                in1=T[g]["dbc"][:].unsqueeze(2).to_broadcast([P, N, 4]),
-                op=ALU.mult,
-            )
-
-        def bmt(g, u):
-            bt = pbt.tile([P, N], F32, tag="bt")
-            T[g]["bt%d" % u] = bt
-            for i in range(NT):
-                nc.tensor.transpose(
-                    bt[:, P * i : P * i + P],
-                    b_sb[:, i, :].bitcast(F32)[:, P * u : P * u + P],
-                    dmf[:, NT * g + i, :],
-                )
-
-        def bme(g, u, copy):
-            if u == 0:
-                bm = work.tile([P, 2, 2 * N], BF16)
+            def copy_bias(g):
+                bm = bias_pool.tile([P, 2, 2 * N], BF16)
                 T[g]["bm"] = bm
-            copy(out=T[g]["bm"][:, u, :].bitcast(F32), in_=T[g]["bt%d" % u][:])
+                for u in range(2):
+                    nc.scalar.copy(out=bm[:, u, :].bitcast(F32), in_=T[g]["bt" + str(u)][:])
 
-        def st_omm(g):
-            for j in range(4):
-                u, h = j // 2, j % 2
-                oj = pmm.tile([P, 2, 256], F32, tag="mm")
-                T[g]["oj%d" % j] = oj
-                cols = slice(256 * h, 256 * h + 256)
-                for e in range(2):
-                    mx(g, oj[:, e, :], "p", slice(P * (2 * u + e), P * (2 * u + e) + P), T[g]["ac"][:, cols], T[g]["as"][:, cols])
+            def product(g):
+                for j in range(4):
+                    u, h = j // 2, j % 2
+                    oj = pmm.tile([P, 2, HALF], F32, tag="mm")
+                    T[g]["oj" + str(j)] = oj
+                    cols = slice(HALF * h, HALF * h + HALF)
+                    for e in range(2):
+                        rows = slice(P * (2 * u + e), P * (2 * u + e) + P)
+                        mx(oj[:, e, :], T[g]["pc"][:, rows], T[g]["ps"][:, rows], T[g]["ac"][:, cols], T[g]["as"][:, cols])
 
-        def st_z(g):
-            for j in range(4):
-                u, h = j // 2, j % 2
-                z = fin.tile([P, 2, 256], F32)
-                T[g]["z%d" % j] = z
-                bias = T[g]["bm"][:, u, :].rearrange("p (n e) -> p e n", e=2)[:, :, 256 * h : 256 * h + 256]
-                nc.vector.tensor_tensor(out=z[:], in0=T[g]["oj%d" % j][:], in1=bias, op=ALU.add)
+            def add_bias(g):
+                for j in range(4):
+                    u, h = j // 2, j % 2
+                    z = zpool.tile([P, 2, HALF], F32)
+                    T[g]["z" + str(j)] = z
+                    bias = T[g]["bm"][:, u, :].rearrange("p (n e) -> p e n", e=2)[:, :, HALF * h : HALF * h + HALF]
+                    nc.vector.tensor_tensor(out=z[:], in0=T[g]["oj" + str(j)][:], in1=bias, op=ALU.add)
 
-        def st_th(g):
-            rows = out[g].rearrange("(u q e) n -> u q e n", u=2, e=2)
-            for j in range(4):
-                u, h = j // 2, j % 2
-                y = fin.tile([P, 2, 256], F32)
-                nc.scalar.activation(out=y[:], in_=T[g]["z%d" % j][:], func=ACT.Tanh)
-                nc.sync.dma_start(out=rows[u][:, :, 256 * h : 256 * h + 256], in_=y[:])
+            def tanh_and_store(g):
+                rows = out[g].rearrange("(u q e) n -> u q e n", u=2, e=2)
+                for j in range(4):
+                    u, h = j // 2, j % 2
+                    y = ypool.tile([P, 2, HALF], F32)
+                    nc.scalar.activation(out=y[:], in_=T[g]["z" + str(j)][:], func=ACT.Tanh)
+                    nc.sync.dma_start(out=rows[u][:, :, HALF * h : HALF * h + HALF], in_=y[:])
 
-        def at(g, stage):
-            if 0 <= g < G:
-                stage(g)
-
-        for s in range(G + 3):
-            at(s - 2, lambda g: bme(g, 0, nc.scalar.copy))
-            at(s - 2, lambda g: st_dch(g))
-            at(s - 3, lambda g: st_th(g))
-            at(s - 1, lambda g: st_xg(g))
-            at(s - 1, lambda g: st_psmm(g))
-            at(s - 2, lambda g: bmt(g, 1))
-            at(s, lambda g: st_trA(g))
-            at(s - 2, lambda g: st_scl(g))
-            at(s, lambda g: fgc(g, 0, nc.vector.tensor_copy))
-            at(s - 1, lambda g: pse(g, (0, 1), nc.scalar.copy))
-            at(s - 1, lambda g: pse(g, (2, 3), nc.scalar.copy))
-            at(s, lambda g: fgc(g, 1, nc.scalar.copy))
-            at(s - 1, lambda g: quantise(g, "xg", "x"))
-            at(s - 2, lambda g: bme(g, 1, nc.vector.tensor_copy))
-            at(s - 2, lambda g: st_dbc(g))
-            at(s - 1, lambda g: quantise(g, "psg", "p"))
-            at(s - 1, lambda g: st_emm(g))
-            at(s, lambda g: st_sq(g))
-            at(s - 2, lambda g: st_p2(g))
-            at(s - 2, lambda g: quantise(g, "ag", "a"))
-            at(s, lambda g: quantise(g, "fg", "f"))
-            at(s - 1, lambda g: bmt(g, 0))
-            at(s - 1, lambda g: st_relu(g))
-            at(s - 2, lambda g: st_omm(g))
-            at(s, lambda g: st_rn(g))
-            at(s, lambda g: st_trM(g))
-            at(s - 1, lambda g: st_diag(g))
-            at(s - 2, lambda g: st_z(g))
+            for s in range(-2, G + 2):
+                at(s + 2, add_identity)
+                at(s + 2, inverse_root_degrees)
+                at(s + 2, scale_rows)
+                at(s, spread_d)
+                at(s, pre_sup)
+                at(s, scale_columns)
+                at(s, copy_bias)
+                at(s + 1, bias_transposes)
+                at(s, copy_pre_sup)
+                at(s, quantise_adj)
+                at(s, quantise_pre_sup)
+                at(s - 1, product)
+                at(s - 1, add_bias)
+                at(s - 2, tanh_and_store)

@@ -17,6 +17,7 @@ N = 512
 D = 512
 NT = N // P
 HALF = N // 2
+EARLY = 4
 FLOPS = 3 * 2 * G * N * N * D
 
 
@@ -60,6 +61,8 @@ def tile_graphlearner_pa_t_kernel(tc, feat, mask, W, b, out):
         wcodes = const.tile([P, D], U32, align_bytes=64)
         wscales = const.tile([P, D], U8, align_bytes=64)
         deg = const.tile([P, G, 2, 8], F32)
+        dv = const.tile([P, G, NT], F32)
+        small = ctx.enter_context(tc.tile_pool(name="small", bufs=2))
         fcodes = []
         fscales = []
         r = []
@@ -70,6 +73,44 @@ def tile_graphlearner_pa_t_kernel(tc, feat, mask, W, b, out):
         T = []
         for g in range(G):
             T.append({})
+
+        def add_identity(g):
+            rdiag = r[g][:].rearrange("p (t s) -> p t s", s=N + P)[:, :, 0:P]
+            nc.gpsimd.tensor_tensor(
+                out=rdiag, in0=rdiag, in1=ident_f[:].unsqueeze(1).to_broadcast([P, 4, P]), op=ALU.add
+            )
+
+        def inverse_root_degrees(g):
+            gs = slice(NT * g, NT * g + NT)
+            dg2 = small.tile([P, 2, 2], F32)
+            nc.gpsimd.tensor_tensor(
+                out=dg2[:],
+                in0=deg[:, g, :, 0:2],
+                in1=maskeps[:, gs].rearrange("p (a c) -> p a c", c=2),
+                op=ALU.add,
+            )
+            nc.gpsimd.tensor_tensor(
+                out=dv[:, g, :], in0=dg2[:].rearrange("p a c -> p (a c)"), in1=neghalf[:], op=ALU.pow
+            )
+
+        def scale_rows(g):
+            for t in range(4):
+                nc.gpsimd.tensor_scalar(
+                    out=r[g][:, N * t : N * t + N],
+                    in0=r[g][:, N * t : N * t + N],
+                    scalar1=dv[:, g, t : t + 1],
+                    scalar2=maskT[:, NT * g + t : NT * g + t + 1],
+                    op0=ALU.mult,
+                    op1=ALU.mult,
+                )
+
+        def normalise_half(k):
+            g, part = divmod(k, 2)
+            if part == 0:
+                add_identity(g)
+                inverse_root_degrees(g)
+            else:
+                scale_rows(g)
 
         with ExitStack() as one:
             big = one.enter_context(tc.tile_pool(name="big", bufs=1))
@@ -212,25 +253,26 @@ def tile_graphlearner_pa_t_kernel(tc, feat, mask, W, b, out):
                         accum_out=deg[:, g, 1, t - 2 : t - 1],
                     )
 
-            for s in range(-3, G + 3):
+            for s in range(-3, G + 4):
                 at(s, copy_features)
                 at(s - 3, relu_scalar)
-                at(s, squares)
-                at(s - 1, masked_transposes)
+                if s == -1:
+                    quantise_w(s)
                 at(s - 2, quantise_normed)
+                at(s, squares)
+                at(s, quantise_features)
                 at(s + 1, plain_transposes)
                 at(s - 3, relu_vector)
-                at(s + 3, masked_identity)
-                at(s, quantise_features)
-                if s == 0:
-                    quantise_w(s)
+                at(s - 1, masked_transposes)
+                if 0 <= s - 4 < 2 * EARLY:
+                    normalise_half(s - 4)
                 at(s - 1, normed_features)
-                at(s, inverse_norms)
                 at(s - 2, edge)
+                at(s, inverse_norms)
+                at(s + 3, masked_identity)
 
         with ExitStack() as two:
             work = two.enter_context(tc.tile_pool(name="work2", bufs=2))
-            small = two.enter_context(tc.tile_pool(name="small", bufs=4))
             bias_pool = two.enter_context(tc.tile_pool(name="bias", bufs=3))
             zpool = two.enter_context(tc.tile_pool(name="zpool", bufs=8))
             ypool = two.enter_context(tc.tile_pool(name="ypool", bufs=4))
@@ -238,45 +280,13 @@ def tile_graphlearner_pa_t_kernel(tc, feat, mask, W, b, out):
             pbt = two.enter_context(tc.psum_pool(name="pbt", bufs=2))
             pdb = two.enter_context(tc.psum_pool(name="pdb", bufs=1))
 
-            def add_identity(g):
-                rdiag = r[g][:].rearrange("p (t s) -> p t s", s=N + P)[:, :, 0:P]
-                nc.gpsimd.tensor_tensor(
-                    out=rdiag, in0=rdiag, in1=ident_f[:].unsqueeze(1).to_broadcast([P, 4, P]), op=ALU.add
-                )
-
-            def inverse_root_degrees(g):
-                gs = slice(NT * g, NT * g + NT)
-                dg2 = small.tile([P, 2, 2], F32)
-                nc.gpsimd.tensor_tensor(
-                    out=dg2[:],
-                    in0=deg[:, g, :, 0:2],
-                    in1=maskeps[:, gs].rearrange("p (a c) -> p a c", c=2),
-                    op=ALU.add,
-                )
-                dv = small.tile([P, 4], F32)
-                T[g]["dv"] = dv
-                nc.gpsimd.tensor_tensor(
-                    out=dv[:], in0=dg2[:].rearrange("p a c -> p (a c)"), in1=neghalf[:], op=ALU.pow
-                )
-
-            def scale_rows(g):
-                for t in range(4):
-                    nc.gpsimd.tensor_scalar(
-                        out=r[g][:, N * t : N * t + N],
-                        in0=r[g][:, N * t : N * t + N],
-                        scalar1=T[g]["dv"][:, t : t + 1],
-                        scalar2=maskT[:, NT * g + t : NT * g + t + 1],
-                        op0=ALU.mult,
-                        op1=ALU.mult,
-                    )
-
             def spread_d(g):
                 dbc = pdb.tile([P, N], F32, tag="db")
                 T[g]["dbc"] = dbc
                 for i in range(NT):
                     nc.tensor.matmul(
                         out=dbc[:, P * i : P * i + P],
-                        lhsT=T[g]["dv"][:, i : i + 1].to_broadcast([P, P]),
+                        lhsT=dv[:, g, i : i + 1].to_broadcast([P, P]),
                         rhs=ident_f[:],
                         start=True,
                         stop=True,
@@ -366,17 +376,18 @@ def tile_graphlearner_pa_t_kernel(tc, feat, mask, W, b, out):
                     nc.sync.dma_start(out=rows[u][:, :, HALF * h : HALF * h + HALF], in_=y[:])
 
             for s in range(-2, G + 2):
-                at(s + 2, add_identity)
-                at(s + 2, inverse_root_degrees)
-                at(s + 2, scale_rows)
+                at(s, copy_bias)
                 at(s, spread_d)
                 at(s, pre_sup)
-                at(s, scale_columns)
-                at(s, copy_bias)
                 at(s + 1, bias_transposes)
+                at(s - 1, product)
+                at(s, scale_columns)
                 at(s, copy_pre_sup)
                 at(s, quantise_adj)
                 at(s, quantise_pre_sup)
-                at(s - 1, product)
                 at(s - 1, add_bias)
                 at(s - 2, tanh_and_store)
+                if s + 2 >= EARLY:
+                    at(s + 2, add_identity)
+                    at(s + 2, inverse_root_degrees)
+                    at(s + 2, scale_rows)

@@ -17,6 +17,7 @@ N = 512
 D = 512
 NT = N // P
 HALF = N // 2
+SCALAR_PLANES = 3
 EARLY = 4
 FLOPS = 3 * 2 * G * N * N * D
 
@@ -60,7 +61,7 @@ def tile_graphlearner_pa_t_kernel(tc, feat, mask, W, b, out):
         b_sb = const.tile([P, NT, D], BF16)
         wcodes = const.tile([P, D], U32, align_bytes=64)
         wscales = const.tile([P, D], U8, align_bytes=64)
-        deg = const.tile([P, G, 2, 8], F32)
+        deg = const.tile([P, G, NT, 8], F32)
         dv = const.tile([P, G, NT], F32)
         small = ctx.enter_context(tc.tile_pool(name="small", bufs=2))
         fcodes = []
@@ -82,15 +83,10 @@ def tile_graphlearner_pa_t_kernel(tc, feat, mask, W, b, out):
 
         def inverse_root_degrees(g):
             gs = slice(NT * g, NT * g + NT)
-            dg2 = small.tile([P, 2, 2], F32)
+            dg2 = small.tile([P, NT], F32)
+            nc.gpsimd.tensor_tensor(out=dg2[:], in0=deg[:, g, :, 0], in1=maskeps[:, gs], op=ALU.add)
             nc.gpsimd.tensor_tensor(
-                out=dg2[:],
-                in0=deg[:, g, :, 0:2],
-                in1=maskeps[:, gs].rearrange("p (a c) -> p a c", c=2),
-                op=ALU.add,
-            )
-            nc.gpsimd.tensor_tensor(
-                out=dv[:, g, :], in0=dg2[:].rearrange("p a c -> p (a c)"), in1=neghalf[:], op=ALU.pow
+                out=dv[:, g, :], in0=dg2[:], in1=neghalf[:], op=ALU.pow
             )
 
         def scale_rows(g):
@@ -233,16 +229,16 @@ def tile_graphlearner_pa_t_kernel(tc, feat, mask, W, b, out):
                     mx(et[:], T[g]["xc"][:, cols], T[g]["xs"][:, cols], T[g]["xc"][:], T[g]["xs"][:])
 
             def relu_scalar(g):
-                for t in range(2):
+                for t in range(SCALAR_PLANES):
                     nc.scalar.activation(
                         out=r[g][:, N * t : N * t + N],
                         in_=T[g]["et" + str(t)][:],
                         func=ACT.Relu,
-                        accum_out=deg[:, g, 0, t : t + 1],
+                        accum_out=deg[:, g, t, 0:1],
                     )
 
             def relu_vector(g):
-                for t in range(2, 4):
+                for t in range(SCALAR_PLANES, NT):
                     nc.vector.tensor_scalar(
                         out=r[g][:, N * t : N * t + N],
                         in0=T[g]["et" + str(t)][:],
@@ -250,7 +246,7 @@ def tile_graphlearner_pa_t_kernel(tc, feat, mask, W, b, out):
                         scalar2=None,
                         op0=ALU.max,
                         op1=ALU.add,
-                        accum_out=deg[:, g, 1, t - 2 : t - 1],
+                        accum_out=deg[:, g, t, 0:1],
                     )
 
             for s in range(-3, G + 4):

@@ -17,7 +17,6 @@ N = 512
 D = 512
 NT = N // P
 HALF = N // 2
-SCALAR_PLANES = 3
 EARLY = 4
 FLOPS = 3 * 2 * G * N * N * D
 
@@ -55,13 +54,15 @@ def tile_graphlearner_pa_t_kernel(tc, feat, mask, W, b, out):
         nc.vector.memset(neghalf[:], -0.5)
         mrows = const.tile([P, P], BF16)
         nc.vector.memset(mrows[:], 0.0)
+        first = const.tile([P, NT], F32)
+        nc.scalar.activation(out=first[:], in_=neghalf[:], func=ACT.Tanh)
         maskT = const.tile([P, G * NT], F32)
         maskeps = const.tile([P, G * NT], F32)
         dmf = const.tile([P, G * NT, P], F32)
         b_sb = const.tile([P, NT, D], BF16)
         wcodes = const.tile([P, D], U32, align_bytes=64)
         wscales = const.tile([P, D], U8, align_bytes=64)
-        deg = const.tile([P, G, NT, 8], F32)
+        deg = const.tile([P, G, 2, 8], F32)
         dv = const.tile([P, G, NT], F32)
         small = ctx.enter_context(tc.tile_pool(name="small", bufs=2))
         fcodes = []
@@ -83,10 +84,15 @@ def tile_graphlearner_pa_t_kernel(tc, feat, mask, W, b, out):
 
         def inverse_root_degrees(g):
             gs = slice(NT * g, NT * g + NT)
-            dg2 = small.tile([P, NT], F32)
-            nc.gpsimd.tensor_tensor(out=dg2[:], in0=deg[:, g, :, 0], in1=maskeps[:, gs], op=ALU.add)
+            dg2 = small.tile([P, 2, 2], F32)
             nc.gpsimd.tensor_tensor(
-                out=dv[:, g, :], in0=dg2[:], in1=neghalf[:], op=ALU.pow
+                out=dg2[:],
+                in0=deg[:, g, :, 0:2],
+                in1=maskeps[:, gs].rearrange("p (a c) -> p a c", c=2),
+                op=ALU.add,
+            )
+            nc.gpsimd.tensor_tensor(
+                out=dv[:, g, :], in0=dg2[:].rearrange("p a c -> p (a c)"), in1=neghalf[:], op=ALU.pow
             )
 
         def scale_rows(g):
@@ -229,16 +235,16 @@ def tile_graphlearner_pa_t_kernel(tc, feat, mask, W, b, out):
                     mx(et[:], T[g]["xc"][:, cols], T[g]["xs"][:, cols], T[g]["xc"][:], T[g]["xs"][:])
 
             def relu_scalar(g):
-                for t in range(SCALAR_PLANES):
+                for t in range(2):
                     nc.scalar.activation(
                         out=r[g][:, N * t : N * t + N],
                         in_=T[g]["et" + str(t)][:],
                         func=ACT.Relu,
-                        accum_out=deg[:, g, t, 0:1],
+                        accum_out=deg[:, g, 0, t : t + 1],
                     )
 
             def relu_vector(g):
-                for t in range(SCALAR_PLANES, NT):
+                for t in range(2, 4):
                     nc.vector.tensor_scalar(
                         out=r[g][:, N * t : N * t + N],
                         in0=T[g]["et" + str(t)][:],
@@ -246,7 +252,7 @@ def tile_graphlearner_pa_t_kernel(tc, feat, mask, W, b, out):
                         scalar2=None,
                         op0=ALU.max,
                         op1=ALU.add,
-                        accum_out=deg[:, g, t, 0:1],
+                        accum_out=deg[:, g, 1, t - 2 : t - 1],
                     )
 
             for s in range(-3, G + 4):
@@ -265,7 +271,8 @@ def tile_graphlearner_pa_t_kernel(tc, feat, mask, W, b, out):
                 at(s - 1, normed_features)
                 at(s - 2, edge)
                 at(s, inverse_norms)
-                at(s + 3, masked_identity)
+                for k in range(3):
+                    at(3 * (s + 3) + k, masked_identity)
 
         with ExitStack() as two:
             work = two.enter_context(tc.tile_pool(name="work2", bufs=2))
@@ -280,13 +287,7 @@ def tile_graphlearner_pa_t_kernel(tc, feat, mask, W, b, out):
                 dbc = pdb.tile([P, N], F32, tag="db")
                 T[g]["dbc"] = dbc
                 for i in range(NT):
-                    nc.tensor.matmul(
-                        out=dbc[:, P * i : P * i + P],
-                        lhsT=dv[:, g, i : i + 1].to_broadcast([P, P]),
-                        rhs=ident_f[:],
-                        start=True,
-                        stop=True,
-                    )
+                    nc.tensor.transpose(dbc[:, P * i : P * i + P], dv[:, g, i : i + 1].to_broadcast([P, P]), ident_f[:])
 
             def pre_sup(g):
                 for j in range(4):

@@ -29,7 +29,7 @@ def tile_graphlearner_pa_t_kernel(tc, feat, mask, W, b, out):
             stage(g)
 
     def quantise(codes, scales, grouped):
-        nc.vector.quantize_mx(out=codes[:].bitcast(FP8X4), scales=scales[:], in_=grouped[:])
+        nc.vector.quantize_mx(out=codes.bitcast(FP8X4), scales=scales, in_=grouped)
 
     def mx(dst, lcodes, lscales, rcodes, rscales):
         nc.tensor.matmul_mx(
@@ -45,11 +45,18 @@ def tile_graphlearner_pa_t_kernel(tc, feat, mask, W, b, out):
     with ExitStack() as ctx:
         ctx.enter_context(tc.manual_schedule())
         const = ctx.enter_context(tc.tile_pool(name="const", bufs=1))
+        feats = ctx.enter_context(tc.tile_pool(name="feats", bufs=6))
+        work = ctx.enter_context(tc.tile_pool(name="work", bufs=2))
+        small = ctx.enter_context(tc.tile_pool(name="small", bufs=3))
+        zpool = ctx.enter_context(tc.tile_pool(name="zpool", bufs=8))
+        ptr = ctx.enter_context(tc.psum_pool(name="ptr", bufs=2))
+        pgr = ctx.enter_context(tc.psum_pool(name="pgr", bufs=2))
+        pmm = ctx.enter_context(tc.psum_pool(name="pmm", bufs=4))
 
-        ident_f = const.tile([P, P], F32)
-        make_identity(nc, ident_f[:])
         ident_b = const.tile([P, P], BF16)
         make_identity(nc, ident_b[:])
+        ident_f = const.tile([P, P], F32)
+        make_identity(nc, ident_f[:])
         neghalf = const.tile([P, NT], F32)
         nc.vector.memset(neghalf[:], -0.5)
         mrows = const.tile([P, P], BF16)
@@ -60,46 +67,172 @@ def tile_graphlearner_pa_t_kernel(tc, feat, mask, W, b, out):
         maskeps = const.tile([P, G * NT], F32)
         dmf = const.tile([P, G * NT, P], F32)
         b_sb = const.tile([P, NT, D], BF16)
+        wraw = const.tile([P, 4, D], BF16)
+        wg = const.tile([P, D * 4], BF16, align_bytes=64)
         wcodes = const.tile([P, D], U32, align_bytes=64)
         wscales = const.tile([P, D], U8, align_bytes=64)
-        deg = const.tile([P, G, 2, 8], F32)
+        deg = const.tile([P, G, NT], F32)
         dv = const.tile([P, G, NT], F32)
-        small = ctx.enter_context(tc.tile_pool(name="small", bufs=2))
-        fcodes = []
-        fscales = []
-        r = []
-        for g in range(G):
-            fcodes.append(const.tile([P, N], U32, align_bytes=64, name="fc%d" % g))
-            fscales.append(const.tile([P, N], U8, align_bytes=64, name="fs%d" % g))
-            r.append(const.tile([P, 5 * N], F32, name="r%d" % g))
+        rall = const.tile([P, 4 * G * N], F32)
+        codes1 = []
+        scales1 = []
+        f_sb = []
         T = []
         for g in range(G):
+            codes1.append(const.tile([P, 2 * N], U32, align_bytes=64, name="c%d" % g))
+            scales1.append(const.tile([P, 2 * N], U8, align_bytes=64, name="s%d" % g))
+            f_sb.append(feats.tile([P, NT, D], BF16, tag="f", name="f%d" % g))
             T.append({})
 
-        def add_identity(g):
-            rdiag = r[g][:].rearrange("p (t s) -> p t s", s=N + P)[:, :, 0:P]
-            nc.gpsimd.tensor_tensor(
-                out=rdiag, in0=rdiag, in1=ident_f[:].unsqueeze(1).to_broadcast([P, 4, P]), op=ALU.add
+        def r(g, t):
+            return rall[:, 4 * N * g + N * t : 4 * N * g + N * t + N]
+
+        nc.sync.dma_start(out=mrows[0 : G * NT, :], in_=mask.rearrange("g (i p) -> (g i) p", p=P))
+
+        def load(g):
+            nc.sync.dma_start(out=f_sb[g][:], in_=feat[g].rearrange("(i p) d -> p i d", p=P))
+
+        load(0)
+        for u in range(2):
+            nc.sync.dma_start(
+                out=wraw[:, 2 * u : 2 * u + 2, :],
+                in_=W[256 * u : 256 * u + 256, :].rearrange("(q e) c -> q e c", e=2),
+            )
+        for g in range(1, 6):
+            load(g)
+
+        mT_ps = ptr.tile([P, P], BF16, tag="tr")
+        nc.tensor.transpose(mT_ps[:], mrows[:], ident_b[:])
+        nc.vector.tensor_copy(out=maskT[:], in_=mT_ps[:, 0 : G * NT])
+        nc.vector.tensor_scalar_add(out=maskeps[:], in0=maskT[:], scalar1=1e-8)
+
+        def masked_identity_vector(g):
+            gs = slice(NT * g, NT * g + NT)
+            nc.vector.tensor_tensor(
+                out=dmf[:, gs, :],
+                in0=ident_f[:].unsqueeze(1).to_broadcast([P, NT, P]),
+                in1=maskT[:, gs].unsqueeze(2).to_broadcast([P, NT, P]),
+                op=ALU.mult,
             )
 
+        def masked_identity_gpsimd(g):
+            for i in range(NT):
+                nc.gpsimd.tensor_scalar(
+                    out=dmf[:, NT * g + i, :],
+                    in0=ident_f[:],
+                    scalar1=maskT[:, NT * g + i : NT * g + i + 1],
+                    scalar2=0.0,
+                    op0=ALU.mult,
+                    op1=ALU.add,
+                )
+
+        def copy_w():
+            for u in range(2):
+                nc.scalar.copy(
+                    out=wg[:].rearrange("p (u e q t) -> p u e q t", u=2, e=2, t=4)[:, u],
+                    in_=wraw[:].rearrange("p t (u q e) -> p u e q t", u=2, e=2)[:, u],
+                )
+
+        def gram(g):
+            gr = pgr.tile([P, 4, P], F32, tag="gr")
+            T[g]["gr"] = gr
+            columns = f_sb[g][:].rearrange("p i (u q e) -> p i u e q", u=2, e=2)
+            for u in range(2):
+                for e in range(2):
+                    for i in range(NT):
+                        block = columns[:, i, u, e, :]
+                        nc.tensor.matmul(gr[:, 2 * u + e, :], lhsT=block, rhs=block, start=(i == 0), stop=(i == NT - 1))
+
+        def diagonals(g):
+            ss = small.tile([P, 4], F32)
+            T[g]["ss"] = ss
+            for t in range(4):
+                junk = small.tile([P, P], F32)
+                nc.vector.scalar_tensor_tensor(
+                    out=junk[:],
+                    in0=T[g]["gr"][:, t, :],
+                    scalar=1.0,
+                    in1=ident_f[:],
+                    op0=ALU.mult,
+                    op1=ALU.mult,
+                    accum_out=ss[:, t : t + 1],
+                )
+
+        def inverse_norms(g):
+            ssm = small.tile([P, 4], F32)
+            nc.gpsimd.tensor_scalar_max(out=ssm[:], in0=T[g]["ss"][:], scalar1=1e-24)
+            rn = small.tile([P, 4], F32)
+            T[g]["rn"] = rn
+            nc.gpsimd.tensor_tensor(out=rn[:], in0=ssm[:], in1=neghalf[:], op=ALU.pow)
+
+        def masked_transposes(g):
+            for h in range(2):
+                ft = ptr.tile([P, 2, HALF], F32, tag="tr")
+                T[g]["ft" + str(h)] = ft
+                for u in range(2):
+                    for ii in range(2):
+                        i = 2 * h + ii
+                        nc.tensor.transpose(
+                            ft[:, u, P * ii : P * ii + P],
+                            f_sb[g][:, i, :].bitcast(F32)[:, P * u : P * u + P],
+                            dmf[:, NT * g + i, :],
+                        )
+
+        def copy_features(g, halves):
+            fg32 = T[g]["fx"][:, 0 : 4 * N].bitcast(F32).rearrange("p (n u) -> p n u", u=2)
+            for h in halves:
+                nc.scalar.copy(
+                    out=fg32[:, HALF * h : HALF * h + HALF, :], in_=T[g]["ft" + str(h)][:].rearrange("p u n -> p n u")
+                )
+
+        def open_first(g):
+            fx = work.tile([P, 2 * N * 4], BF16, align_bytes=64)
+            T[g]["fx"] = fx
+
+        def normed_features(g, halves):
+            xg4 = T[g]["fx"][:, 4 * N : 8 * N].rearrange("p (n u e) -> p n u e", u=2, e=2)
+            for h in halves:
+                nc.vector.tensor_tensor(
+                    out=xg4[:, HALF * h : HALF * h + HALF, :, :],
+                    in0=T[g]["ft" + str(h)][:]
+                    .rearrange("p u n -> p (u n)")
+                    .bitcast(BF16)
+                    .rearrange("p (u n e) -> p n u e", u=2, e=2),
+                    in1=T[g]["rn"][:].rearrange("p (u e) -> p u e", e=2).unsqueeze(1).to_broadcast([P, HALF, 2, 2]),
+                    op=ALU.mult,
+                )
+
+        def quantise_features(g):
+            quantise(codes1[g][:], scales1[g][:], T[g]["fx"][:])
+
+        def edge(g):
+            xc = codes1[g][:, N : 2 * N]
+            xs = scales1[g][:, N : 2 * N]
+            for t in range(4):
+                et = pmm.tile([P, N], F32, tag="mm")
+                T[g]["et" + str(t)] = et
+                cols = slice(P * t, P * t + P)
+                mx(et[:], xc[:, cols], xs[:, cols], xc, xs)
+
+        def relu(g, planes=range(4)):
+            for t in planes:
+                nc.scalar.activation(out=r(g, t), in_=T[g]["et" + str(t)][:], func=ACT.Relu, accum_out=deg[:, g, t : t + 1])
+
+        def add_identity(g):
+            for t in range(4):
+                block = r(g, t)[:, P * t : P * t + P]
+                nc.gpsimd.tensor_tensor(out=block, in0=block, in1=ident_f[:], op=ALU.add)
+
         def inverse_root_degrees(g):
-            gs = slice(NT * g, NT * g + NT)
-            dg2 = small.tile([P, 2, 2], F32)
-            nc.gpsimd.tensor_tensor(
-                out=dg2[:],
-                in0=deg[:, g, :, 0:2],
-                in1=maskeps[:, gs].rearrange("p (a c) -> p a c", c=2),
-                op=ALU.add,
-            )
-            nc.gpsimd.tensor_tensor(
-                out=dv[:, g, :], in0=dg2[:].rearrange("p a c -> p (a c)"), in1=neghalf[:], op=ALU.pow
-            )
+            dg2 = small.tile([P, NT], F32)
+            nc.gpsimd.tensor_tensor(out=dg2[:], in0=deg[:, g, :], in1=maskeps[:, NT * g : NT * g + NT], op=ALU.add)
+            nc.gpsimd.tensor_tensor(out=dv[:, g, :], in0=dg2[:], in1=neghalf[:], op=ALU.pow)
 
         def scale_rows(g):
             for t in range(4):
                 nc.gpsimd.tensor_scalar(
-                    out=r[g][:, N * t : N * t + N],
-                    in0=r[g][:, N * t : N * t + N],
+                    out=r(g, t),
+                    in0=r(g, t),
                     scalar1=dv[:, g, t : t + 1],
                     scalar2=maskT[:, NT * g + t : NT * g + t + 1],
                     op0=ALU.mult,
@@ -114,277 +247,154 @@ def tile_graphlearner_pa_t_kernel(tc, feat, mask, W, b, out):
             else:
                 scale_rows(g)
 
-        with ExitStack() as one:
-            big = one.enter_context(tc.tile_pool(name="big", bufs=1))
-            work = one.enter_context(tc.tile_pool(name="work", bufs=3))
-            ptr = one.enter_context(tc.psum_pool(name="ptr", bufs=4))
-            pmm = one.enter_context(tc.psum_pool(name="pmm", bufs=4))
+        def spread_d(g):
+            dbc = pgr.tile([P, N], F32, tag="gr")
+            T[g]["dbc"] = dbc
+            for i in range(NT):
+                nc.tensor.transpose(dbc[:, P * i : P * i + P], dv[:, g, i : i + 1].to_broadcast([P, P]), ident_f[:])
 
-            f_sb = []
-            for g in range(G):
-                f_sb.append(big.tile([P, NT, D], BF16, name="f%d" % g))
-            wraw = big.tile([P, 4, D], BF16)
-            wg = big.tile([P, D * 4], BF16, align_bytes=64)
+        def pre_sup(g, blocks=range(4)):
+            for j in blocks:
+                pj = pmm.tile([P, 4, P], F32, tag="mm")
+                T[g]["pj" + str(j)] = pj
+                cols = slice(P * j, P * j + P)
+                for t in range(4):
+                    rows = slice(P * t, P * t + P)
+                    mx(pj[:, t, :], codes1[g][:, rows], scales1[g][:, rows], wcodes[:, cols], wscales[:, cols])
 
-            nc.sync.dma_start(out=mrows[0 : G * NT, :], in_=mask.rearrange("g (i p) -> (g i) p", p=P))
-            nc.sync.dma_start(out=f_sb[0][:], in_=feat[0].rearrange("(i p) d -> p i d", p=P))
+        def copy_pre_sup(g, blocks=range(4)):
+            psg3 = T[g]["ap"][:, 4 * N : 8 * N].rearrange("p (e t) -> p e t", t=4)
+            for j in blocks:
+                nc.scalar.copy(out=psg3[:, P * j : P * j + P, :], in_=T[g]["pj" + str(j)][:].rearrange("p t e -> p e t"))
+
+        def open_second(g):
+            ap = work.tile([P, 2 * N * 4], BF16, align_bytes=64)
+            T[g]["ap"] = ap
+
+        def scale_columns(g):
+            ap = T[g]["ap"]
+            nc.vector.tensor_tensor(
+                out=ap[:, 0 : 4 * N].rearrange("p (n t) -> p n t", t=4),
+                in0=rall[:, 4 * N * g : 4 * N * g + 4 * N].rearrange("p (t n) -> p n t", t=4),
+                in1=T[g]["dbc"][:].unsqueeze(2).to_broadcast([P, N, 4]),
+                op=ALU.mult,
+            )
+
+        def quantise_second(g):
+            c2 = work.tile([P, 2 * N], U32, align_bytes=64)
+            s2 = work.tile([P, 2 * N], U8, align_bytes=64)
+            T[g]["c2"] = c2
+            T[g]["s2"] = s2
+            quantise(c2[:], s2[:], T[g]["ap"][:])
+
+        def bias_transposes(g):
             for u in range(2):
-                nc.sync.dma_start(
-                    out=wraw[:, 2 * u : 2 * u + 2, :],
-                    in_=W[256 * u : 256 * u + 256, :].rearrange("(q e) c -> q e c", e=2),
-                )
-            for g in range(1, G):
-                nc.sync.dma_start(out=f_sb[g][:], in_=feat[g].rearrange("(i p) d -> p i d", p=P))
-            nc.sync.dma_start(out=b_sb[:], in_=b.rearrange("(i p) e -> p i e", p=P))
-
-            mT_ps = ptr.tile([P, P], BF16, tag="tr")
-            nc.tensor.transpose(mT_ps[:], mrows[:], ident_b[:])
-            nc.vector.tensor_copy(out=maskT[:], in_=mT_ps[:, 0 : G * NT])
-            nc.vector.tensor_scalar_add(out=maskeps[:], in0=maskT[:], scalar1=1e-8)
-
-            def masked_identity(g):
-                gs = slice(NT * g, NT * g + NT)
-                nc.vector.tensor_tensor(
-                    out=dmf[:, gs, :],
-                    in0=ident_f[:].unsqueeze(1).to_broadcast([P, NT, P]),
-                    in1=maskT[:, gs].unsqueeze(2).to_broadcast([P, NT, P]),
-                    op=ALU.mult,
-                )
-
-            def quantise_w(g):
-                for u in range(2):
-                    nc.vector.tensor_copy(
-                        out=wg[:].rearrange("p (u e q t) -> p u e q t", u=2, e=2, t=4)[:, u],
-                        in_=wraw[:].rearrange("p t (u q e) -> p u e q t", u=2, e=2)[:, u],
-                    )
-                quantise(wcodes, wscales, wg)
-
-            def words(g, i, u):
-                return f_sb[g][:, i, :].bitcast(F32)[:, P * u : P * u + P]
-
-            def transposes(g, key, identity_of):
-                for h in range(2):
-                    ft = ptr.tile([P, 2, HALF], F32, tag="tr")
-                    T[g][key + str(h)] = ft
-                    for u in range(2):
-                        for ii in range(2):
-                            nc.tensor.transpose(
-                                ft[:, u, P * ii : P * ii + P], words(g, 2 * h + ii, u), identity_of(2 * h + ii)
-                            )
-
-            def plain_transposes(g):
-                transposes(g, "ft", lambda i: ident_f[:])
-
-            def masked_transposes(g):
-                transposes(g, "fm", lambda i: dmf[:, NT * g + i, :])
-
-            def copy_features(g):
-                fg = work.tile([P, N * 4], BF16, align_bytes=64)
-                T[g]["fg"] = fg
-                fg32 = fg[:].bitcast(F32).rearrange("p (n u) -> p n u", u=2)
-                for h in range(2):
-                    nc.scalar.copy(
-                        out=fg32[:, HALF * h : HALF * h + HALF, :], in_=T[g]["ft" + str(h)][:].rearrange("p u n -> p n u")
-                    )
-
-            def squares(g):
-                ss = work.tile([P, 4], F32)
-                T[g]["ss"] = ss
-                fg3 = T[g]["fg"][:].rearrange("p (n t) -> p n t", t=4)
-                for t in range(4):
-                    junk = work.tile([P, N], BF16)
-                    nc.scalar.activation(out=junk[:], in_=fg3[:, :, t], func=ACT.Square, accum_out=ss[:, t : t + 1])
-
-            def inverse_norms(g):
-                ssm = work.tile([P, 4], F32)
-                nc.gpsimd.tensor_scalar_max(out=ssm[:], in0=T[g]["ss"][:], scalar1=1e-24)
-                rn = work.tile([P, 4], F32)
-                T[g]["rn"] = rn
-                nc.gpsimd.tensor_tensor(out=rn[:], in0=ssm[:], in1=neghalf[:], op=ALU.pow)
-
-            def quantise_features(g):
-                quantise(fcodes[g], fscales[g], T[g]["fg"])
-
-            def normed_features(g):
-                xg = work.tile([P, N * 4], BF16, align_bytes=64)
-                T[g]["xg"] = xg
-                xg4 = xg[:].rearrange("p (n u e) -> p n u e", u=2, e=2)
-                for h in range(2):
-                    nc.vector.tensor_tensor(
-                        out=xg4[:, HALF * h : HALF * h + HALF, :, :],
-                        in0=T[g]["fm" + str(h)][:]
-                        .rearrange("p u n -> p (u n)")
-                        .bitcast(BF16)
-                        .rearrange("p (u n e) -> p n u e", u=2, e=2),
-                        in1=T[g]["rn"][:].rearrange("p (u e) -> p u e", e=2).unsqueeze(1).to_broadcast([P, HALF, 2, 2]),
-                        op=ALU.mult,
-                    )
-
-            def quantise_normed(g):
-                xc = work.tile([P, N], U32, align_bytes=64)
-                xs = work.tile([P, N], U8, align_bytes=64)
-                T[g]["xc"] = xc
-                T[g]["xs"] = xs
-                quantise(xc, xs, T[g]["xg"])
-
-            def edge(g):
-                for t in range(4):
-                    et = pmm.tile([P, N], F32, tag="mm")
-                    T[g]["et" + str(t)] = et
-                    cols = slice(P * t, P * t + P)
-                    mx(et[:], T[g]["xc"][:, cols], T[g]["xs"][:, cols], T[g]["xc"][:], T[g]["xs"][:])
-
-            def relu_scalar(g):
-                for t in range(2):
-                    nc.scalar.activation(
-                        out=r[g][:, N * t : N * t + N],
-                        in_=T[g]["et" + str(t)][:],
-                        func=ACT.Relu,
-                        accum_out=deg[:, g, 0, t : t + 1],
-                    )
-
-            def relu_vector(g):
-                for t in range(2, 4):
-                    nc.vector.tensor_scalar(
-                        out=r[g][:, N * t : N * t + N],
-                        in0=T[g]["et" + str(t)][:],
-                        scalar1=0.0,
-                        scalar2=None,
-                        op0=ALU.max,
-                        op1=ALU.add,
-                        accum_out=deg[:, g, 1, t - 2 : t - 1],
-                    )
-
-            for s in range(-3, G + 4):
-                at(s, copy_features)
-                at(s - 3, relu_scalar)
-                if s == -1:
-                    quantise_w(s)
-                at(s - 2, quantise_normed)
-                at(s, squares)
-                at(s, quantise_features)
-                at(s + 1, plain_transposes)
-                at(s - 3, relu_vector)
-                at(s - 1, masked_transposes)
-                if 0 <= s - 4 < 2 * EARLY:
-                    normalise_half(s - 4)
-                at(s - 1, normed_features)
-                at(s - 2, edge)
-                at(s, inverse_norms)
-                for k in range(3):
-                    at(3 * (s + 3) + k, masked_identity)
-
-        with ExitStack() as two:
-            work = two.enter_context(tc.tile_pool(name="work2", bufs=2))
-            bias_pool = two.enter_context(tc.tile_pool(name="bias", bufs=3))
-            zpool = two.enter_context(tc.tile_pool(name="zpool", bufs=8))
-            ypool = two.enter_context(tc.tile_pool(name="ypool", bufs=4))
-            pmm = two.enter_context(tc.psum_pool(name="pmm2", bufs=5))
-            pbt = two.enter_context(tc.psum_pool(name="pbt", bufs=2))
-            pdb = two.enter_context(tc.psum_pool(name="pdb", bufs=1))
-
-            def spread_d(g):
-                dbc = pdb.tile([P, N], F32, tag="db")
-                T[g]["dbc"] = dbc
+                bt = ptr.tile([P, N], F32, tag="tr")
+                T[g]["bt" + str(u)] = bt
                 for i in range(NT):
-                    nc.tensor.transpose(dbc[:, P * i : P * i + P], dv[:, g, i : i + 1].to_broadcast([P, P]), ident_f[:])
+                    nc.tensor.transpose(
+                        bt[:, P * i : P * i + P],
+                        b_sb[:, i, :].bitcast(F32)[:, P * u : P * u + P],
+                        dmf[:, NT * g + i, :],
+                    )
 
-            def pre_sup(g):
-                for j in range(4):
-                    pj = pmm.tile([P, 4, P], F32, tag="mm")
-                    T[g]["pj" + str(j)] = pj
-                    cols = slice(P * j, P * j + P)
-                    for t in range(4):
-                        rows = slice(P * t, P * t + P)
-                        mx(pj[:, t, :], fcodes[g][:, rows], fscales[g][:, rows], wcodes[:, cols], wscales[:, cols])
+        def copy_bias(g):
+            bm = work.tile([P, 2, 2 * N], BF16)
+            T[g]["bm"] = bm
+            for u in range(2):
+                nc.scalar.copy(out=bm[:, u, :].bitcast(F32), in_=T[g]["bt" + str(u)][:])
 
-            def copy_pre_sup(g):
-                psg = work.tile([P, D * 4], BF16, align_bytes=64)
-                T[g]["psg"] = psg
-                psg3 = psg[:].rearrange("p (e t) -> p e t", t=4)
-                for j in range(4):
-                    nc.scalar.copy(out=psg3[:, P * j : P * j + P, :], in_=T[g]["pj" + str(j)][:].rearrange("p t e -> p e t"))
+        def product(g):
+            c2 = T[g]["c2"]
+            s2 = T[g]["s2"]
+            for j in range(4):
+                u, h = j // 2, j % 2
+                oj = pmm.tile([P, 2, HALF], F32, tag="mm")
+                T[g]["oj" + str(j)] = oj
+                cols = slice(HALF * h, HALF * h + HALF)
+                for e in range(2):
+                    rows = slice(N + P * (2 * u + e), N + P * (2 * u + e) + P)
+                    mx(oj[:, e, :], c2[:, rows], s2[:, rows], c2[:, cols], s2[:, cols])
 
-            def quantise_pre_sup(g):
-                pc = work.tile([P, D], U32, align_bytes=64)
-                ps = work.tile([P, D], U8, align_bytes=64)
-                T[g]["pc"] = pc
-                T[g]["ps"] = ps
-                quantise(pc, ps, T[g]["psg"])
+        def add_bias(g):
+            for j in range(4):
+                u, h = j // 2, j % 2
+                z = zpool.tile([P, 2, HALF], F32)
+                T[g]["z" + str(j)] = z
+                bias = T[g]["bm"][:, u, :].rearrange("p (n e) -> p e n", e=2)[:, :, HALF * h : HALF * h + HALF]
+                nc.vector.tensor_tensor(out=z[:], in0=T[g]["oj" + str(j)][:], in1=bias, op=ALU.add)
 
-            def scale_columns(g):
-                adjg = work.tile([P, N * 4], BF16, align_bytes=64)
-                T[g]["ag"] = adjg
-                nc.vector.tensor_tensor(
-                    out=adjg[:].rearrange("p (n t) -> p n t", t=4),
-                    in0=r[g][:, 0 : 4 * N].rearrange("p (t n) -> p n t", t=4),
-                    in1=T[g]["dbc"][:].unsqueeze(2).to_broadcast([P, N, 4]),
-                    op=ALU.mult,
-                )
+        def tanh_and_store(g):
+            rows = out[g].rearrange("(u q e) n -> u q e n", u=2, e=2)
+            for j in range(4):
+                u, h = j // 2, j % 2
+                z = T[g]["z" + str(j)]
+                nc.scalar.activation(out=z[:], in_=z[:], func=ACT.Tanh)
+                nc.sync.dma_start(out=rows[u][:, :, HALF * h : HALF * h + HALF], in_=z[:])
 
-            def quantise_adj(g):
-                ac = work.tile([P, N], U32, align_bytes=64)
-                asc = work.tile([P, N], U8, align_bytes=64)
-                T[g]["ac"] = ac
-                T[g]["as"] = asc
-                quantise(ac, asc, T[g]["ag"])
-
-            def bias_transposes(g):
-                for u in range(2):
-                    bt = pbt.tile([P, N], F32, tag="bt")
-                    T[g]["bt" + str(u)] = bt
-                    for i in range(NT):
-                        nc.tensor.transpose(
-                            bt[:, P * i : P * i + P],
-                            b_sb[:, i, :].bitcast(F32)[:, P * u : P * u + P],
-                            dmf[:, NT * g + i, :],
-                        )
-
-            def copy_bias(g):
-                bm = bias_pool.tile([P, 2, 2 * N], BF16)
-                T[g]["bm"] = bm
-                for u in range(2):
-                    nc.scalar.copy(out=bm[:, u, :].bitcast(F32), in_=T[g]["bt" + str(u)][:])
-
-            def product(g):
-                for j in range(4):
-                    u, h = j // 2, j % 2
-                    oj = pmm.tile([P, 2, HALF], F32, tag="mm")
-                    T[g]["oj" + str(j)] = oj
-                    cols = slice(HALF * h, HALF * h + HALF)
-                    for e in range(2):
-                        rows = slice(P * (2 * u + e), P * (2 * u + e) + P)
-                        mx(oj[:, e, :], T[g]["pc"][:, rows], T[g]["ps"][:, rows], T[g]["ac"][:, cols], T[g]["as"][:, cols])
-
-            def add_bias(g):
-                for j in range(4):
-                    u, h = j // 2, j % 2
-                    z = zpool.tile([P, 2, HALF], F32)
-                    T[g]["z" + str(j)] = z
-                    bias = T[g]["bm"][:, u, :].rearrange("p (n e) -> p e n", e=2)[:, :, HALF * h : HALF * h + HALF]
-                    nc.vector.tensor_tensor(out=z[:], in0=T[g]["oj" + str(j)][:], in1=bias, op=ALU.add)
-
-            def tanh_and_store(g):
-                rows = out[g].rearrange("(u q e) n -> u q e n", u=2, e=2)
-                for j in range(4):
-                    u, h = j // 2, j % 2
-                    y = ypool.tile([P, 2, HALF], F32)
-                    nc.scalar.activation(out=y[:], in_=T[g]["z" + str(j)][:], func=ACT.Tanh)
-                    nc.sync.dma_start(out=rows[u][:, :, HALF * h : HALF * h + HALF], in_=y[:])
-
-            for s in range(-2, G + 2):
-                at(s, copy_bias)
-                at(s, spread_d)
-                at(s, pre_sup)
-                at(s + 1, bias_transposes)
-                at(s - 1, product)
-                at(s, scale_columns)
-                at(s, copy_pre_sup)
-                at(s, quantise_adj)
-                at(s, quantise_pre_sup)
-                at(s - 1, add_bias)
-                at(s - 2, tanh_and_store)
-                if s + 2 >= EARLY:
-                    at(s + 2, add_identity)
-                    at(s + 2, inverse_root_degrees)
-                    at(s + 2, scale_rows)
+        ahead = {2: 0, 3: 1, 4: 2, 5: 3}
+        open_second(0)
+        masked_identity_vector(0)
+        for s in range(-2, 2 * G):
+            k = s - (G - 1)
+            if 0 <= s < G:
+                open_first(s)
+                normed_features(s, [0])
+            at(s + 1, diagonals)
+            at(s + 1, inverse_norms)
+            if 0 <= s < G:
+                normed_features(s, [1])
+            if s == -1:
+                copy_w()
+            if 0 <= s - 2 < G - 1:
+                relu(s - 2, [0, 1])
+            if 0 <= s < G:
+                copy_features(s, [0])
+            if 0 <= s - 2 < G - 1:
+                relu(s - 2, [2, 3])
+            if 0 <= s < G:
+                copy_features(s, [1])
+            at(s - 1, quantise_features)
+            if s == 0:
+                quantise(wcodes[:], wscales[:], wg[:])
+                load(6)
+                load(7)
+                nc.sync.dma_start(out=b_sb[:], in_=b.rearrange("(i p) e -> p i e", p=P))
+            at(s + 2, gram)
+            at(s + 1, masked_transposes)
+            if s in ahead:
+                pre_sup(0, [ahead[s]])
+                copy_pre_sup(0, [ahead[s]])
+            if s == 7:
+                spread_d(0)
+                bias_transposes(0)
+                copy_bias(0)
+            at(s - 1, edge)
+            if 1 <= s + 3 < G:
+                masked_identity_gpsimd(s + 3)
+            if 0 <= s - 3 < 2 * EARLY:
+                normalise_half(s - 3)
+            if k >= 3 and EARLY + k - 3 < G:
+                add_identity(EARLY + k - 3)
+                inverse_root_degrees(EARLY + k - 3)
+                scale_rows(EARLY + k - 3)
+            if k == 1:
+                relu(G - 1)
+                quantise_second(0)
+                product(0)
+                pre_sup(1)
+            at(k, scale_columns)
+            if k >= 1:
+                at(k, copy_pre_sup)
+                at(k, copy_bias)
+                at(k - 1, add_bias)
+                at(k, quantise_second)
+                at(k - 1, tanh_and_store)
+            if k >= 0:
+                at(k + 1, open_second)
+                at(k + 1, spread_d)
+                at(k + 1, bias_transposes)
+                if k >= 1:
+                    at(k + 1, pre_sup)
+            if k >= 1:
+                at(k, product)

@@ -73,7 +73,7 @@ def tile_graphlearner_pa_t_kernel(tc, feat, mask, W, b, out):
         wscales = const.tile([P, D], U8, align_bytes=64)
         deg = const.tile([P, G, NT], F32)
         dv = const.tile([P, G, NT], F32)
-        rall = const.tile([P, 4 * G * N], F32)
+        rall = const.tile([P, (4 * G + 1) * N], F32)
         codes1 = []
         scales1 = []
         f_sb = []
@@ -115,15 +115,13 @@ def tile_graphlearner_pa_t_kernel(tc, feat, mask, W, b, out):
                 op=ALU.mult,
             )
 
-        def masked_identity_gpsimd(g):
+        def masked_identity_scalar(g):
             for i in range(NT):
-                nc.gpsimd.tensor_scalar(
+                nc.scalar.activation(
                     out=dmf[:, NT * g + i, :],
-                    in0=ident_f[:],
-                    scalar1=maskT[:, NT * g + i : NT * g + i + 1],
-                    scalar2=0.0,
-                    op0=ALU.mult,
-                    op1=ALU.add,
+                    in_=ident_f[:],
+                    func=ACT.Copy,
+                    scale=maskT[:, NT * g + i : NT * g + i + 1],
                 )
 
         def copy_w():
@@ -219,9 +217,10 @@ def tile_graphlearner_pa_t_kernel(tc, feat, mask, W, b, out):
                 nc.scalar.activation(out=r(g, t), in_=T[g]["et" + str(t)][:], func=ACT.Relu, accum_out=deg[:, g, t : t + 1])
 
         def add_identity(g):
-            for t in range(4):
-                block = r(g, t)[:, P * t : P * t + P]
-                nc.gpsimd.tensor_tensor(out=block, in0=block, in1=ident_f[:], op=ALU.add)
+            rdiag = rall[:, 4 * N * g : 4 * N * g + 5 * N].rearrange("p (t s) -> p t s", s=N + P)[:, :, 0:P]
+            nc.gpsimd.tensor_tensor(
+                out=rdiag, in0=rdiag, in1=ident_f[:].unsqueeze(1).to_broadcast([P, 4, P]), op=ALU.add
+            )
 
         def inverse_root_degrees(g):
             dg2 = small.tile([P, NT], F32)
@@ -334,14 +333,23 @@ def tile_graphlearner_pa_t_kernel(tc, feat, mask, W, b, out):
 
         ahead = {2: 0, 3: 1, 4: 2, 5: 3}
         open_second(0)
-        masked_identity_vector(0)
+        for g in range(3):
+            masked_identity_vector(g)
+        for g in range(3, G):
+            masked_identity_scalar(g)
         for s in range(-2, 2 * G):
             k = s - (G - 1)
+            if s in ahead:
+                pre_sup(0, [ahead[s]])
             if 0 <= s < G:
                 open_first(s)
                 normed_features(s, [0])
-            at(s + 1, diagonals)
-            at(s + 1, inverse_norms)
+            if s < 1:
+                at(s + 1, diagonals)
+                at(s + 1, inverse_norms)
+            else:
+                at(s + 2, diagonals)
+                at(s + 2, inverse_norms)
             if 0 <= s < G:
                 normed_features(s, [1])
             if s == -1:
@@ -356,22 +364,30 @@ def tile_graphlearner_pa_t_kernel(tc, feat, mask, W, b, out):
                 copy_features(s, [1])
             at(s - 1, quantise_features)
             if s == 0:
+                gram(2)
+                diagonals(2)
+                inverse_norms(2)
+            if s == 0:
                 quantise(wcodes[:], wscales[:], wg[:])
                 load(6)
                 load(7)
                 nc.sync.dma_start(out=b_sb[:], in_=b.rearrange("(i p) e -> p i e", p=P))
-            at(s + 2, gram)
+            if s == -2:
+                gram(0)
+            if s >= 1:
+                at(s + 3, gram)
             at(s + 1, masked_transposes)
+            if s == -1:
+                gram(1)
+            if s == 0:
+                gram(3)
             if s in ahead:
-                pre_sup(0, [ahead[s]])
                 copy_pre_sup(0, [ahead[s]])
             if s == 7:
                 spread_d(0)
                 bias_transposes(0)
                 copy_bias(0)
             at(s - 1, edge)
-            if 1 <= s + 3 < G:
-                masked_identity_gpsimd(s + 3)
             if 0 <= s - 3 < 2 * EARLY:
                 normalise_half(s - 3)
             if k >= 3 and EARLY + k - 3 < G:

@@ -48,7 +48,8 @@ def tile_graphlearner_pa_t_kernel(tc, feat, mask, W, b, out):
         feats = ctx.enter_context(tc.tile_pool(name="feats", bufs=6))
         work = ctx.enter_context(tc.tile_pool(name="work", bufs=2))
         small = ctx.enter_context(tc.tile_pool(name="small", bufs=3))
-        zpool = ctx.enter_context(tc.tile_pool(name="zpool", bufs=8))
+        fxpool = ctx.enter_context(tc.tile_pool(name="fxpool", bufs=3))
+        zpool = ctx.enter_context(tc.tile_pool(name="zpool", bufs=6))
         ptr = ctx.enter_context(tc.psum_pool(name="ptr", bufs=2))
         pgr = ctx.enter_context(tc.psum_pool(name="pgr", bufs=2))
         pmm = ctx.enter_context(tc.psum_pool(name="pmm", bufs=4))
@@ -163,8 +164,8 @@ def tile_graphlearner_pa_t_kernel(tc, feat, mask, W, b, out):
             T[g]["rn"] = rn
             nc.gpsimd.tensor_tensor(out=rn[:], in0=ssm[:], in1=neghalf[:], op=ALU.pow)
 
-        def masked_transposes(g):
-            for h in range(2):
+        def masked_transposes(g, halves=range(2)):
+            for h in halves:
                 ft = ptr.tile([P, 2, HALF], F32, tag="tr")
                 T[g]["ft" + str(h)] = ft
                 for u in range(2):
@@ -184,7 +185,7 @@ def tile_graphlearner_pa_t_kernel(tc, feat, mask, W, b, out):
                 )
 
         def open_first(g):
-            fx = work.tile([P, 2 * N * 4], BF16, align_bytes=64)
+            fx = fxpool.tile([P, 2 * N * 4], BF16, align_bytes=64)
             T[g]["fx"] = fx
 
         def normed_features(g, halves):
@@ -273,9 +274,9 @@ def tile_graphlearner_pa_t_kernel(tc, feat, mask, W, b, out):
         def scale_columns(g):
             ap = T[g]["ap"]
             nc.vector.tensor_tensor(
-                out=ap[:, 0 : 4 * N].rearrange("p (n t) -> p n t", t=4),
-                in0=rall[:, 4 * N * g : 4 * N * g + 4 * N].rearrange("p (t n) -> p n t", t=4),
-                in1=T[g]["dbc"][:].unsqueeze(2).to_broadcast([P, N, 4]),
+                out=ap[:, 0 : 4 * N].rearrange("p (c i t) -> p c t i", i=4, t=4),
+                in0=rall[:, 4 * N * g : 4 * N * g + 4 * N].rearrange("p (t c i) -> p c t i", t=4, i=4),
+                in1=T[g]["dbc"][:].rearrange("p (c i) -> p c i", i=4).unsqueeze(2).to_broadcast([P, P, 4, 4]),
                 op=ALU.mult,
             )
 
@@ -286,9 +287,9 @@ def tile_graphlearner_pa_t_kernel(tc, feat, mask, W, b, out):
             T[g]["s2"] = s2
             quantise(c2[:], s2[:], T[g]["ap"][:])
 
-        def bias_transposes(g):
-            for u in range(2):
-                bt = ptr.tile([P, N], F32, tag="tr")
+        def bias_transposes(g, words=range(2)):
+            for u in words:
+                bt = pgr.tile([P, N], F32, tag="gr")
                 T[g]["bt" + str(u)] = bt
                 for i in range(NT):
                     nc.tensor.transpose(
@@ -297,120 +298,130 @@ def tile_graphlearner_pa_t_kernel(tc, feat, mask, W, b, out):
                         dmf[:, NT * g + i, :],
                     )
 
-        def copy_bias(g):
+        def open_bias(g):
             bm = work.tile([P, 2, 2 * N], BF16)
             T[g]["bm"] = bm
-            for u in range(2):
+
+        def copy_bias(g, words=range(2)):
+            bm = T[g]["bm"]
+            for u in words:
                 nc.scalar.copy(out=bm[:, u, :].bitcast(F32), in_=T[g]["bt" + str(u)][:])
 
-        def product(g):
+        def product(g, banks=range(4)):
             c2 = T[g]["c2"]
             s2 = T[g]["s2"]
-            for j in range(4):
+            for j in banks:
                 u, h = j // 2, j % 2
-                oj = pmm.tile([P, 2, HALF], F32, tag="mm")
+                oj = ptr.tile([P, 2, HALF], F32, tag="tr")
                 T[g]["oj" + str(j)] = oj
                 cols = slice(HALF * h, HALF * h + HALF)
                 for e in range(2):
                     rows = slice(N + P * (2 * u + e), N + P * (2 * u + e) + P)
                     mx(oj[:, e, :], c2[:, rows], s2[:, rows], c2[:, cols], s2[:, cols])
 
-        def add_bias(g):
-            for j in range(4):
+        def add_bias(g, banks=range(4)):
+            for j in banks:
                 u, h = j // 2, j % 2
                 z = zpool.tile([P, 2, HALF], F32)
                 T[g]["z" + str(j)] = z
                 bias = T[g]["bm"][:, u, :].rearrange("p (n e) -> p e n", e=2)[:, :, HALF * h : HALF * h + HALF]
                 nc.vector.tensor_tensor(out=z[:], in0=T[g]["oj" + str(j)][:], in1=bias, op=ALU.add)
 
-        def tanh_and_store(g):
+        def tanh_and_store(g, banks=range(4)):
             rows = out[g].rearrange("(u q e) n -> u q e n", u=2, e=2)
-            for j in range(4):
+            for j in banks:
                 u, h = j // 2, j % 2
                 z = T[g]["z" + str(j)]
                 nc.scalar.activation(out=z[:], in_=z[:], func=ACT.Tanh)
                 nc.sync.dma_start(out=rows[u][:, :, HALF * h : HALF * h + HALF], in_=z[:])
 
-        ahead = {2: 0, 3: 1, 4: 2, 5: 3}
-        open_second(0)
         for g in range(3):
             masked_identity_vector(g)
         for g in range(3, G):
             masked_identity_scalar(g)
-        for s in range(-2, 2 * G):
-            k = s - (G - 1)
-            if s in ahead:
-                pre_sup(0, [ahead[s]])
-            if 0 <= s < G:
-                open_first(s)
-                normed_features(s, [0])
-            if s < 1:
-                at(s + 1, diagonals)
-                at(s + 1, inverse_norms)
-            else:
-                at(s + 2, diagonals)
-                at(s + 2, inverse_norms)
-            if 0 <= s < G:
-                normed_features(s, [1])
-            if s == -1:
-                copy_w()
-            if 0 <= s - 2 < G - 1:
-                relu(s - 2, [0, 1])
-            if 0 <= s < G:
-                copy_features(s, [0])
-            if 0 <= s - 2 < G - 1:
-                relu(s - 2, [2, 3])
-            if 0 <= s < G:
-                copy_features(s, [1])
-            at(s - 1, quantise_features)
+        gram(0)
+        masked_transposes(0)
+        diagonals(0)
+        inverse_norms(0)
+        copy_w()
+        gram(1)
+        for s in range(G):
+            if 3 <= s < 7:
+                pre_sup(0, [s - 3])
+            if s >= 1:
+                at(s + 2, gram)
+                masked_transposes(s, [1])
+            open_first(s)
             if s == 0:
-                gram(2)
-                diagonals(2)
-                inverse_norms(2)
-            if s == 0:
+                normed_features(0, [0, 1])
                 quantise(wcodes[:], wscales[:], wg[:])
                 load(6)
                 load(7)
                 nc.sync.dma_start(out=b_sb[:], in_=b.rearrange("(i p) e -> p i e", p=P))
-            if s == -2:
-                gram(0)
-            if s >= 1:
-                at(s + 3, gram)
-            at(s + 1, masked_transposes)
-            if s == -1:
-                gram(1)
+            at(s + 1, diagonals)
+            at(s + 1, inverse_norms)
+            if s >= 3:
+                relu(s - 3, [2, 3])
+            if s == 2:
+                open_second(0)
+            if 3 <= s < 7:
+                copy_pre_sup(0, [s - 3])
+            if s >= 2:
+                quantise_features(s - 2)
+                edge(s - 2)
+                relu(s - 2, [0])
+            if s > 0:
+                normed_features(s, [0, 1])
+            copy_features(s, [0])
             if s == 0:
-                gram(3)
-            if s in ahead:
-                copy_pre_sup(0, [ahead[s]])
-            if s == 7:
-                spread_d(0)
-                bias_transposes(0)
-                copy_bias(0)
-            at(s - 1, edge)
+                gram(2)
+            if s + 1 < G:
+                masked_transposes(s + 1, [0])
+            if s >= 2:
+                relu(s - 2, [1])
+            copy_features(s, [1])
             if 0 <= s - 3 < 2 * EARLY:
                 normalise_half(s - 3)
-            if k >= 3 and EARLY + k - 3 < G:
-                add_identity(EARLY + k - 3)
-                inverse_root_degrees(EARLY + k - 3)
-                scale_rows(EARLY + k - 3)
-            if k == 1:
-                relu(G - 1)
-                quantise_second(0)
-                product(0)
-                pre_sup(1)
-            at(k, scale_columns)
-            if k >= 1:
-                at(k, copy_pre_sup)
-                at(k, copy_bias)
-                at(k - 1, add_bias)
-                at(k, quantise_second)
-                at(k - 1, tanh_and_store)
-            if k >= 0:
-                at(k + 1, open_second)
-                at(k + 1, spread_d)
-                at(k + 1, bias_transposes)
-                if k >= 1:
-                    at(k + 1, pre_sup)
-            if k >= 1:
-                at(k, product)
+        for h in range(5, 8):
+            normalise_half(h)
+        open_bias(0)
+        spread_d(0)
+        bias_transposes(0, [0])
+        scale_columns(0)
+        relu(G - 3, [2, 3])
+        copy_bias(0, [0])
+        bias_transposes(0, [1])
+        copy_bias(0, [1])
+        quantise_features(G - 2)
+        edge(G - 2)
+        spread_d(1)
+        relu(G - 2)
+        quantise_second(0)
+        product(0, [0, 1])
+        pre_sup(1)
+        for k in range(1, G + 1):
+            if k < G:
+                open_second(k)
+                open_bias(k)
+                scale_columns(k)
+                bias_transposes(k, [0])
+                copy_pre_sup(k)
+                if k == 1:
+                    quantise_features(G - 1)
+                    edge(G - 1)
+                    relu(G - 1)
+                bias_transposes(k, [1])
+                copy_bias(k)
+            add_bias(k - 1, [0, 1])
+            product(k - 1, [2, 3])
+            at(k + 1, pre_sup)
+            at(k + 1, spread_d)
+            add_bias(k - 1, [2, 3])
+            tanh_and_store(k - 1)
+            if k < G:
+                quantise_second(k)
+                product(k, [0, 1])
+            if EARLY + k - 1 < G:
+                add_identity(EARLY + k - 1)
+                inverse_root_degrees(EARLY + k - 1)
+                scale_rows(EARLY + k - 1)

@@ -17,7 +17,6 @@ N = 512
 D = 512
 NT = N // P
 HALF = N // 2
-EARLY = 4
 FLOPS = 3 * 2 * G * N * N * D
 
 
@@ -43,33 +42,25 @@ def tile_graphlearner_pa_t_kernel(tc, feat, mask, W, b, out):
         )
 
     with ExitStack() as ctx:
-        ctx.enter_context(tc.manual_schedule())
         const = ctx.enter_context(tc.tile_pool(name="const", bufs=1))
-        feats = ctx.enter_context(tc.tile_pool(name="feats", bufs=6))
+        feats = ctx.enter_context(tc.tile_pool(name="feats", bufs=5))
         work = ctx.enter_context(tc.tile_pool(name="work", bufs=2))
         small = ctx.enter_context(tc.tile_pool(name="small", bufs=3))
         fxpool = ctx.enter_context(tc.tile_pool(name="fxpool", bufs=3))
-        zpool = ctx.enter_context(tc.tile_pool(name="zpool", bufs=6))
+        bpool = ctx.enter_context(tc.tile_pool(name="bpool", bufs=3))
+        zpool = ctx.enter_context(tc.tile_pool(name="zpool", bufs=8))
         ptr = ctx.enter_context(tc.psum_pool(name="ptr", bufs=2))
-        pgr = ctx.enter_context(tc.psum_pool(name="pgr", bufs=2))
+        pone = ctx.enter_context(tc.psum_pool(name="pone", bufs=1))
         pmm = ctx.enter_context(tc.psum_pool(name="pmm", bufs=4))
 
         ident_b = const.tile([P, P], BF16)
-        make_identity(nc, ident_b[:])
         ident_f = const.tile([P, P], F32)
-        make_identity(nc, ident_f[:])
         neghalf = const.tile([P, NT], F32)
-        nc.vector.memset(neghalf[:], -0.5)
         mrows = const.tile([P, P], BF16)
-        nc.vector.memset(mrows[:], 0.0)
         first = const.tile([P, NT], F32)
-        nc.scalar.activation(out=first[:], in_=neghalf[:], func=ACT.Tanh)
         maskT = const.tile([P, G * NT], F32)
-        maskeps = const.tile([P, G * NT], F32)
         dmf = const.tile([P, G * NT, P], F32)
         b_sb = const.tile([P, NT, D], BF16)
-        wraw = const.tile([P, 4, D], BF16)
-        wg = const.tile([P, D * 4], BF16, align_bytes=64)
         wcodes = const.tile([P, D], U32, align_bytes=64)
         wscales = const.tile([P, D], U8, align_bytes=64)
         deg = const.tile([P, G, NT], F32)
@@ -88,24 +79,33 @@ def tile_graphlearner_pa_t_kernel(tc, feat, mask, W, b, out):
         def r(g, t):
             return rall[:, 4 * N * g + N * t : 4 * N * g + N * t + N]
 
-        nc.sync.dma_start(out=mrows[0 : G * NT, :], in_=mask.rearrange("g (i p) -> (g i) p", p=P))
+        wboth = fxpool.tile([P, 2 * N * 4], BF16, align_bytes=64, tag="fx")
+        wraw = wboth[:, 0 : 4 * D].rearrange("p (t c) -> p t c", t=4)
+        wg = wboth[:, 4 * D : 8 * D]
 
         def load(g):
             nc.sync.dma_start(out=f_sb[g][:], in_=feat[g].rearrange("(i p) d -> p i d", p=P))
 
-        load(0)
-        for u in range(2):
-            nc.sync.dma_start(
-                out=wraw[:, 2 * u : 2 * u + 2, :],
-                in_=W[256 * u : 256 * u + 256, :].rearrange("(q e) c -> q e c", e=2),
-            )
-        for g in range(1, 6):
-            load(g)
-
-        mT_ps = ptr.tile([P, P], BF16, tag="tr")
-        nc.tensor.transpose(mT_ps[:], mrows[:], ident_b[:])
-        nc.vector.tensor_copy(out=maskT[:], in_=mT_ps[:, 0 : G * NT])
-        nc.vector.tensor_scalar_add(out=maskeps[:], in0=maskT[:], scalar1=1e-8)
+        def constants_and_loads():
+            make_identity(nc, ident_b[:])
+            make_identity(nc, ident_f[:])
+            nc.vector.memset(neghalf[:], -0.5)
+            nc.vector.memset(mrows[:], 0.0)
+            nc.scalar.activation(out=first[:], in_=neghalf[:], func=ACT.Abs_reciprocal_sqrt)
+            nc.sync.dma_start(out=mrows[0 : G * NT, :], in_=mask.rearrange("g (i p) -> (g i) p", p=P))
+            load(0)
+            for u in range(2):
+                nc.sync.dma_start(
+                    out=wraw[:, 2 * u : 2 * u + 2, :],
+                    in_=W[256 * u : 256 * u + 256, :].rearrange("(q e) c -> q e c", e=2),
+                )
+            load(1)
+            nc.sync.dma_start(out=b_sb[:], in_=b.rearrange("(i p) e -> p i e", p=P))
+            for g in range(2, 5):
+                load(g)
+            mT_ps = ptr.tile([P, P], BF16, tag="tr")
+            nc.tensor.transpose(mT_ps[:], mrows[:], ident_b[:])
+            nc.vector.tensor_copy(out=maskT[:], in_=mT_ps[:, 0 : G * NT])
 
         def masked_identity_vector(g):
             gs = slice(NT * g, NT * g + NT)
@@ -128,12 +128,12 @@ def tile_graphlearner_pa_t_kernel(tc, feat, mask, W, b, out):
         def copy_w():
             for u in range(2):
                 nc.scalar.copy(
-                    out=wg[:].rearrange("p (u e q t) -> p u e q t", u=2, e=2, t=4)[:, u],
-                    in_=wraw[:].rearrange("p t (u q e) -> p u e q t", u=2, e=2)[:, u],
+                    out=wg.rearrange("p (u e q t) -> p u e q t", u=2, e=2, t=4)[:, u],
+                    in_=wraw.rearrange("p t (u q e) -> p u e q t", u=2, e=2)[:, u],
                 )
 
         def gram(g):
-            gr = pgr.tile([P, 4, P], F32, tag="gr")
+            gr = pone.tile([P, 4, P], F32, tag="ab"[g % 2])
             T[g]["gr"] = gr
             columns = f_sb[g][:].rearrange("p i (u q e) -> p i u e q", u=2, e=2)
             for u in range(2):
@@ -157,12 +157,15 @@ def tile_graphlearner_pa_t_kernel(tc, feat, mask, W, b, out):
                     accum_out=ss[:, t : t + 1],
                 )
 
-        def inverse_norms(g):
+        def clamp_norms(g):
             ssm = small.tile([P, 4], F32)
-            nc.gpsimd.tensor_scalar_max(out=ssm[:], in0=T[g]["ss"][:], scalar1=1e-24)
+            T[g]["ssm"] = ssm
+            nc.vector.tensor_scalar_max(out=ssm[:], in0=T[g]["ss"][:], scalar1=1e-24)
+
+        def inverse_norms(g):
             rn = small.tile([P, 4], F32)
             T[g]["rn"] = rn
-            nc.gpsimd.tensor_tensor(out=rn[:], in0=ssm[:], in1=neghalf[:], op=ALU.pow)
+            nc.scalar.activation(out=rn[:], in_=T[g]["ssm"][:], func=ACT.Abs_reciprocal_sqrt)
 
         def masked_transposes(g, halves=range(2)):
             for h in halves:
@@ -185,7 +188,7 @@ def tile_graphlearner_pa_t_kernel(tc, feat, mask, W, b, out):
                 )
 
         def open_first(g):
-            fx = fxpool.tile([P, 2 * N * 4], BF16, align_bytes=64)
+            fx = fxpool.tile([P, 2 * N * 4], BF16, align_bytes=64, tag="fx")
             T[g]["fx"] = fx
 
         def normed_features(g, halves):
@@ -224,9 +227,12 @@ def tile_graphlearner_pa_t_kernel(tc, feat, mask, W, b, out):
             )
 
         def inverse_root_degrees(g):
-            dg2 = small.tile([P, NT], F32)
-            nc.gpsimd.tensor_tensor(out=dg2[:], in0=deg[:, g, :], in1=maskeps[:, NT * g : NT * g + NT], op=ALU.add)
-            nc.gpsimd.tensor_tensor(out=dv[:, g, :], in0=dg2[:], in1=neghalf[:], op=ALU.pow)
+            if g < G - 1:
+                nc.scalar.activation(out=dv[:, g, :], in_=deg[:, g, :], func=ACT.Abs_reciprocal_sqrt, bias=1.00000001)
+            else:
+                dg2 = small.tile([P, NT], F32)
+                nc.gpsimd.tensor_scalar_add(out=dg2[:], in0=deg[:, g, :], scalar1=1.00000001)
+                nc.gpsimd.tensor_tensor(out=dv[:, g, :], in0=dg2[:], in1=neghalf[:], op=ALU.pow)
 
         def scale_rows(g):
             for t in range(4):
@@ -239,23 +245,22 @@ def tile_graphlearner_pa_t_kernel(tc, feat, mask, W, b, out):
                     op1=ALU.mult,
                 )
 
-        def normalise_half(k):
-            g, part = divmod(k, 2)
-            if part == 0:
-                add_identity(g)
-                inverse_root_degrees(g)
-            else:
-                scale_rows(g)
+        def normalise(g):
+            add_identity(g)
+            scale_rows(g)
 
         def spread_d(g):
-            dbc = pgr.tile([P, N], F32, tag="gr")
+            dbc = pone.tile([P, N], F32, tag="a")
             T[g]["dbc"] = dbc
             for i in range(NT):
                 nc.tensor.transpose(dbc[:, P * i : P * i + P], dv[:, g, i : i + 1].to_broadcast([P, P]), ident_f[:])
 
-        def pre_sup(g, blocks=range(4)):
+        def pre_sup(g, blocks, early=False):
             for j in blocks:
-                pj = pmm.tile([P, 4, P], F32, tag="mm")
+                if early:
+                    pj = pmm.tile([P, 4, P], F32, tag="mm")
+                else:
+                    pj = ptr.tile([P, 4, P], F32, tag="tr")
                 T[g]["pj" + str(j)] = pj
                 cols = slice(P * j, P * j + P)
                 for t in range(4):
@@ -287,9 +292,12 @@ def tile_graphlearner_pa_t_kernel(tc, feat, mask, W, b, out):
             T[g]["s2"] = s2
             quantise(c2[:], s2[:], T[g]["ap"][:])
 
-        def bias_transposes(g, words=range(2)):
+        def bias_transposes(g, words, early=False):
             for u in words:
-                bt = pgr.tile([P, N], F32, tag="gr")
+                if early:
+                    bt = pmm.tile([P, N], F32, tag="mm")
+                else:
+                    bt = pone.tile([P, N], F32, tag="b")
                 T[g]["bt" + str(u)] = bt
                 for i in range(NT):
                     nc.tensor.transpose(
@@ -299,7 +307,7 @@ def tile_graphlearner_pa_t_kernel(tc, feat, mask, W, b, out):
                     )
 
         def open_bias(g):
-            bm = work.tile([P, 2, 2 * N], BF16)
+            bm = bpool.tile([P, 2, 2 * N], BF16)
             T[g]["bm"] = bm
 
         def copy_bias(g, words=range(2)):
@@ -312,7 +320,7 @@ def tile_graphlearner_pa_t_kernel(tc, feat, mask, W, b, out):
             s2 = T[g]["s2"]
             for j in banks:
                 u, h = j // 2, j % 2
-                oj = ptr.tile([P, 2, HALF], F32, tag="tr")
+                oj = pmm.tile([P, 2, HALF], F32, tag="mm")
                 T[g]["oj" + str(j)] = oj
                 cols = slice(HALF * h, HALF * h + HALF)
                 for e in range(2):
@@ -335,19 +343,9 @@ def tile_graphlearner_pa_t_kernel(tc, feat, mask, W, b, out):
                 nc.scalar.activation(out=z[:], in_=z[:], func=ACT.Tanh)
                 nc.sync.dma_start(out=rows[u][:, :, HALF * h : HALF * h + HALF], in_=z[:])
 
-        for g in range(3):
-            masked_identity_vector(g)
-        for g in range(3, G):
-            masked_identity_scalar(g)
-        gram(0)
-        masked_transposes(0)
-        diagonals(0)
-        inverse_norms(0)
-        copy_w()
-        gram(1)
-        for s in range(G):
+        def first_round(s):
             if 3 <= s < 7:
-                pre_sup(0, [s - 3])
+                pre_sup(0, [s - 3], early=True)
             if s >= 1:
                 at(s + 2, gram)
                 masked_transposes(s, [1])
@@ -355,20 +353,27 @@ def tile_graphlearner_pa_t_kernel(tc, feat, mask, W, b, out):
             if s == 0:
                 normed_features(0, [0, 1])
                 quantise(wcodes[:], wscales[:], wg[:])
+                load(5)
                 load(6)
                 load(7)
-                nc.sync.dma_start(out=b_sb[:], in_=b.rearrange("(i p) e -> p i e", p=P))
-            at(s + 1, diagonals)
-            at(s + 1, inverse_norms)
+            if s + 1 < G:
+                diagonals(s + 1)
+                if s < 2:
+                    clamp_norms(s + 1)
             if s >= 3:
                 relu(s - 3, [2, 3])
+                inverse_root_degrees(s - 3)
+                normalise(s - 3)
             if s == 2:
                 open_second(0)
             if 3 <= s < 7:
                 copy_pre_sup(0, [s - 3])
             if s >= 2:
                 quantise_features(s - 2)
+                at(s + 1, clamp_norms)
                 edge(s - 2)
+            at(s + 1, inverse_norms)
+            if s >= 2:
                 relu(s - 2, [0])
             if s > 0:
                 normed_features(s, [0, 1])
@@ -380,48 +385,94 @@ def tile_graphlearner_pa_t_kernel(tc, feat, mask, W, b, out):
             if s >= 2:
                 relu(s - 2, [1])
             copy_features(s, [1])
-            if 0 <= s - 3 < 2 * EARLY:
-                normalise_half(s - 3)
-        for h in range(5, 8):
-            normalise_half(h)
-        open_bias(0)
+            if s < 2:
+                open_bias(s)
+                bias_transposes(s, [0, 1], early=True)
+                copy_bias(s)
+        with tc.manual_schedule():
+            constants_and_loads()
+            masked_identity_vector(0)
+            gram(0)
+            masked_transposes(0)
+        with tc.manual_schedule(engines={mybir.EngineType.DVE, mybir.EngineType.Pool, mybir.EngineType.SP, mybir.EngineType.PE}):
+            masked_identity_vector(1)
+            masked_identity_vector(2)
+            diagonals(0)
+            clamp_norms(0)
+            inverse_norms(0)
+            for g in range(3, G):
+                masked_identity_scalar(g)
+            copy_w()
+            gram(1)
+            for s in range(3):
+                first_round(s)
+        ctx.enter_context(tc.manual_schedule(engines={mybir.EngineType.DVE, mybir.EngineType.Pool, mybir.EngineType.SP}))
+        for s in range(3, G):
+            first_round(s)
         spread_d(0)
-        bias_transposes(0, [0])
         scale_columns(0)
         relu(G - 3, [2, 3])
-        copy_bias(0, [0])
-        bias_transposes(0, [1])
-        copy_bias(0, [1])
+        inverse_root_degrees(G - 3)
+        normalise(G - 3)
+        open_bias(2)
+        bias_transposes(2, [0])
+        pre_sup(1, [0, 1])
+        copy_bias(2, [0])
+        open_second(1)
+        copy_pre_sup(1, [0, 1])
         quantise_features(G - 2)
         edge(G - 2)
-        spread_d(1)
+        pre_sup(1, [2, 3])
         relu(G - 2)
+        inverse_root_degrees(G - 2)
+        normalise(G - 2)
         quantise_second(0)
-        product(0, [0, 1])
-        pre_sup(1)
-        for k in range(1, G + 1):
+        spread_d(1)
+        bias_transposes(2, [1])
+        product(0)
+        copy_pre_sup(1, [2, 3])
+        scale_columns(1)
+        copy_bias(2, [1])
+        quantise_features(G - 1)
+        add_bias(0)
+        edge(G - 1)
+        relu(G - 1)
+        inverse_root_degrees(G - 1)
+        normalise(G - 1)
+        quantise_second(1)
+        tanh_and_store(0)
+        spread_d(2)
+        pre_sup(2, [0, 1])
+        product(1)
+        for k in range(2, G + 1):
             if k < G:
                 open_second(k)
-                open_bias(k)
                 scale_columns(k)
-                bias_transposes(k, [0])
-                copy_pre_sup(k)
-                if k == 1:
-                    quantise_features(G - 1)
-                    edge(G - 1)
-                    relu(G - 1)
-                bias_transposes(k, [1])
-                copy_bias(k)
-            add_bias(k - 1, [0, 1])
-            product(k - 1, [2, 3])
-            at(k + 1, pre_sup)
-            at(k + 1, spread_d)
-            add_bias(k - 1, [2, 3])
-            tanh_and_store(k - 1)
+                copy_pre_sup(k, [0])
+                pre_sup(k, [2])
+                if k > 2:
+                    copy_bias(k, [0])
+                    bias_transposes(k, [1])
+                copy_pre_sup(k, [1])
+                pre_sup(k, [3])
+                if k > 2:
+                    copy_bias(k, [1])
+                at(k + 1, spread_d)
+                if k + 1 < G:
+                    open_bias(k + 1)
+                    bias_transposes(k + 1, [0])
+                copy_pre_sup(k, [2])
+                if k + 1 < G:
+                    pre_sup(k + 1, [0])
+            add_bias(k - 1, [0])
+            tanh_and_store(k - 1, [0])
+            if k < G:
+                copy_pre_sup(k, [3])
+                if k + 1 < G:
+                    pre_sup(k + 1, [1])
+            for j in range(1, 4):
+                add_bias(k - 1, [j])
+                tanh_and_store(k - 1, [j])
             if k < G:
                 quantise_second(k)
-                product(k, [0, 1])
-            if EARLY + k - 1 < G:
-                add_identity(EARLY + k - 1)
-                inverse_root_degrees(EARLY + k - 1)
-                scale_rows(EARLY + k - 1)
+                product(k)

@@ -45,9 +45,9 @@ def tile_graphlearner_pa_t_kernel(tc, feat, mask, W, b, out):
         const = ctx.enter_context(tc.tile_pool(name="const", bufs=1))
         feats = ctx.enter_context(tc.tile_pool(name="feats", bufs=5))
         work = ctx.enter_context(tc.tile_pool(name="work", bufs=2))
-        small = ctx.enter_context(tc.tile_pool(name="small", bufs=3))
+        small = ctx.enter_context(tc.tile_pool(name="small", bufs=4))
         fxpool = ctx.enter_context(tc.tile_pool(name="fxpool", bufs=3))
-        bpool = ctx.enter_context(tc.tile_pool(name="bpool", bufs=3))
+        bpool = ctx.enter_context(tc.tile_pool(name="bpool", bufs=4))
         zpool = ctx.enter_context(tc.tile_pool(name="zpool", bufs=8))
         ptr = ctx.enter_context(tc.psum_pool(name="ptr", bufs=2))
         pone = ctx.enter_context(tc.psum_pool(name="pone", bufs=1))
@@ -116,21 +116,28 @@ def tile_graphlearner_pa_t_kernel(tc, feat, mask, W, b, out):
                 op=ALU.mult,
             )
 
-        def masked_identity_scalar(g):
+        def masked_identity_gpsimd(g):
             for i in range(NT):
-                nc.scalar.activation(
+                nc.gpsimd.tensor_scalar(
                     out=dmf[:, NT * g + i, :],
-                    in_=ident_f[:],
-                    func=ACT.Copy,
-                    scale=maskT[:, NT * g + i : NT * g + i + 1],
+                    in0=ident_f[:],
+                    scalar1=maskT[:, NT * g + i : NT * g + i + 1],
+                    scalar2=0.0,
+                    op0=ALU.mult,
+                    op1=ALU.add,
                 )
 
         def copy_w():
             for u in range(2):
-                nc.scalar.copy(
-                    out=wg.rearrange("p (u e q t) -> p u e q t", u=2, e=2, t=4)[:, u],
-                    in_=wraw.rearrange("p t (u q e) -> p u e q t", u=2, e=2)[:, u],
-                )
+                for e in range(2):
+                    nc.gpsimd.tensor_scalar(
+                        out=wg.rearrange("p (u e q t) -> p u e q t", u=2, e=2, t=4)[:, u, e],
+                        in0=wraw.rearrange("p t (u q e) -> p u e q t", u=2, e=2)[:, u, e],
+                        scalar1=1.0,
+                        scalar2=0.0,
+                        op0=ALU.mult,
+                        op1=ALU.add,
+                    )
 
         def gram(g):
             gr = pone.tile([P, 4, P], F32, tag="ab"[g % 2])
@@ -169,7 +176,10 @@ def tile_graphlearner_pa_t_kernel(tc, feat, mask, W, b, out):
 
         def masked_transposes(g, halves=range(2)):
             for h in halves:
-                ft = ptr.tile([P, 2, HALF], F32, tag="tr")
+                if g == 1:
+                    ft = pmm.tile([P, 2, HALF], F32, tag="mm")
+                else:
+                    ft = ptr.tile([P, 2, HALF], F32, tag="tr")
                 T[g]["ft" + str(h)] = ft
                 for u in range(2):
                     for ii in range(2):
@@ -180,7 +190,7 @@ def tile_graphlearner_pa_t_kernel(tc, feat, mask, W, b, out):
                             dmf[:, NT * g + i, :],
                         )
 
-        def copy_features(g, halves):
+        def copy_features(g, halves=range(2)):
             fg32 = T[g]["fx"][:, 0 : 4 * N].bitcast(F32).rearrange("p (n u) -> p n u", u=2)
             for h in halves:
                 nc.scalar.copy(
@@ -191,7 +201,7 @@ def tile_graphlearner_pa_t_kernel(tc, feat, mask, W, b, out):
             fx = fxpool.tile([P, 2 * N * 4], BF16, align_bytes=64, tag="fx")
             T[g]["fx"] = fx
 
-        def normed_features(g, halves):
+        def normed_features(g, halves=range(2)):
             xg4 = T[g]["fx"][:, 4 * N : 8 * N].rearrange("p (n u e) -> p n u e", u=2, e=2)
             for h in halves:
                 nc.vector.tensor_tensor(
@@ -201,6 +211,16 @@ def tile_graphlearner_pa_t_kernel(tc, feat, mask, W, b, out):
                     .bitcast(BF16)
                     .rearrange("p (u n e) -> p n u e", u=2, e=2),
                     in1=T[g]["rn"][:].rearrange("p (u e) -> p u e", e=2).unsqueeze(1).to_broadcast([P, HALF, 2, 2]),
+                    op=ALU.mult,
+                )
+
+        def normed_features_gpsimd(g):
+            for c in range(4):
+                cols = slice(N * c, N * c + N)
+                nc.gpsimd.tensor_tensor(
+                    out=T[g]["fx"][:, 4 * N : 8 * N][:, cols].rearrange("p (n t) -> p n t", t=4),
+                    in0=T[g]["fx"][:, cols].rearrange("p (n t) -> p n t", t=4),
+                    in1=T[g]["rn"][:].unsqueeze(1).to_broadcast([P, P, 4]),
                     op=ALU.mult,
                 )
 
@@ -255,7 +275,7 @@ def tile_graphlearner_pa_t_kernel(tc, feat, mask, W, b, out):
             for i in range(NT):
                 nc.tensor.transpose(dbc[:, P * i : P * i + P], dv[:, g, i : i + 1].to_broadcast([P, P]), ident_f[:])
 
-        def pre_sup(g, blocks, early=False):
+        def pre_sup(g, blocks=range(4), early=False):
             for j in blocks:
                 if early:
                     pj = pmm.tile([P, 4, P], F32, tag="mm")
@@ -276,21 +296,25 @@ def tile_graphlearner_pa_t_kernel(tc, feat, mask, W, b, out):
             ap = work.tile([P, 2 * N * 4], BF16, align_bytes=64)
             T[g]["ap"] = ap
 
-        def scale_columns(g):
-            ap = T[g]["ap"]
+        def scale_columns(g, lo=0, hi=N):
+            n4 = (hi - lo) // 4
             nc.vector.tensor_tensor(
-                out=ap[:, 0 : 4 * N].rearrange("p (c i t) -> p c t i", i=4, t=4),
-                in0=rall[:, 4 * N * g : 4 * N * g + 4 * N].rearrange("p (t c i) -> p c t i", t=4, i=4),
-                in1=T[g]["dbc"][:].rearrange("p (c i) -> p c i", i=4).unsqueeze(2).to_broadcast([P, P, 4, 4]),
+                out=T[g]["ap"][:, 4 * lo : 4 * hi].rearrange("p (c i t) -> p c t i", i=4, t=4),
+                in0=rall[:, 4 * N * g : 4 * N * g + 4 * N]
+                .rearrange("p (t n) -> p t n", t=4)[:, :, lo:hi]
+                .rearrange("p t (c i) -> p c t i", i=4),
+                in1=T[g]["dbc"][:, lo:hi].rearrange("p (c i) -> p c i", i=4).unsqueeze(2).to_broadcast([P, n4, 4, 4]),
                 op=ALU.mult,
             )
 
-        def quantise_second(g):
+        def open_codes(g):
             c2 = work.tile([P, 2 * N], U32, align_bytes=64)
             s2 = work.tile([P, 2 * N], U8, align_bytes=64)
             T[g]["c2"] = c2
             T[g]["s2"] = s2
-            quantise(c2[:], s2[:], T[g]["ap"][:])
+
+        def quantise_second(g, lo=0, hi=2 * N):
+            quantise(T[g]["c2"][:, lo:hi], T[g]["s2"][:, lo:hi], T[g]["ap"][:, 4 * lo : 4 * hi])
 
         def bias_transposes(g, words, early=False):
             for u in words:
@@ -343,136 +367,130 @@ def tile_graphlearner_pa_t_kernel(tc, feat, mask, W, b, out):
                 nc.scalar.activation(out=z[:], in_=z[:], func=ACT.Tanh)
                 nc.sync.dma_start(out=rows[u][:, :, HALF * h : HALF * h + HALF], in_=z[:])
 
+        bias_at = {1: 0, 2: 1, 4: 2, 6: 3}
+
         def first_round(s):
-            if 3 <= s < 7:
-                pre_sup(0, [s - 3], early=True)
-            if s >= 1:
-                at(s + 2, gram)
-                masked_transposes(s, [1])
             open_first(s)
-            if s == 0:
-                normed_features(0, [0, 1])
-                quantise(wcodes[:], wscales[:], wg[:])
-                load(5)
-                load(6)
-                load(7)
-            if s + 1 < G:
-                diagonals(s + 1)
-                if s < 2:
-                    clamp_norms(s + 1)
-            if s >= 3:
-                relu(s - 3, [2, 3])
-                inverse_root_degrees(s - 3)
-                normalise(s - 3)
-            if s == 2:
-                open_second(0)
-            if 3 <= s < 7:
-                copy_pre_sup(0, [s - 3])
+            at(s + 1, diagonals)
+            if s < 3:
+                at(s + 2, gram)
             if s >= 2:
                 quantise_features(s - 2)
-                at(s + 1, clamp_norms)
                 edge(s - 2)
+            at(s + 1, clamp_norms)
             at(s + 1, inverse_norms)
+            normed_features(s)
+            copy_features(s)
+            at(s + 1, masked_transposes)
             if s >= 2:
-                relu(s - 2, [0])
-            if s > 0:
-                normed_features(s, [0, 1])
-            copy_features(s, [0])
-            if s == 0:
-                gram(2)
-            if s + 1 < G:
-                masked_transposes(s + 1, [0])
-            if s >= 2:
-                relu(s - 2, [1])
-            copy_features(s, [1])
-            if s < 2:
-                open_bias(s)
-                bias_transposes(s, [0, 1], early=True)
-                copy_bias(s)
-        with tc.manual_schedule():
-            constants_and_loads()
-            masked_identity_vector(0)
-            gram(0)
-            masked_transposes(0)
-        with tc.manual_schedule(engines={mybir.EngineType.DVE, mybir.EngineType.Pool, mybir.EngineType.SP, mybir.EngineType.PE}):
-            masked_identity_vector(1)
-            masked_identity_vector(2)
-            diagonals(0)
-            clamp_norms(0)
-            inverse_norms(0)
-            for g in range(3, G):
-                masked_identity_scalar(g)
-            copy_w()
-            gram(1)
-            for s in range(3):
+                relu(s - 2)
+                inverse_root_degrees(s - 2)
+                normalise(s - 2)
+            if s >= 3:
+                at(s + 2, gram)
+            if 3 <= s < 7:
+                if s == 3:
+                    open_second(0)
+                pre_sup(0, [s - 3], early=True)
+                copy_pre_sup(0, [s - 3])
+            if s in bias_at:
+                open_bias(bias_at[s])
+                bias_transposes(bias_at[s], [0, 1], early=True)
+                copy_bias(bias_at[s])
+
+        ctx.enter_context(
+            tc.manual_schedule(engines={mybir.EngineType.DVE, mybir.EngineType.Pool, mybir.EngineType.SP})
+        )
+        with tc.manual_schedule(engines={mybir.EngineType.PE}):
+            with tc.manual_schedule(engines={mybir.EngineType.Activation}):
+                constants_and_loads()
+                for g in range(3):
+                    masked_identity_vector(g)
+                masked_identity_gpsimd(3)
+                copy_w()
+                for g in range(4, G):
+                    masked_identity_gpsimd(g)
+                gram(0)
+                masked_transposes(0)
+                gram(1)
+                masked_transposes(1)
+                diagonals(0)
+                clamp_norms(0)
+                inverse_norms(0)
+                open_first(0)
+                normed_features(0)
+                copy_features(0)
+                diagonals(1)
+                clamp_norms(1)
+                inverse_norms(1)
+            gram(2)
+            quantise(wcodes[:], wscales[:], wg[:])
+            load(5)
+            load(6)
+            load(7)
+            for s in range(1, 3):
                 first_round(s)
-        ctx.enter_context(tc.manual_schedule(engines={mybir.EngineType.DVE, mybir.EngineType.Pool, mybir.EngineType.SP}))
         for s in range(3, G):
             first_round(s)
         spread_d(0)
         scale_columns(0)
-        relu(G - 3, [2, 3])
-        inverse_root_degrees(G - 3)
-        normalise(G - 3)
-        open_bias(2)
-        bias_transposes(2, [0])
-        pre_sup(1, [0, 1])
-        copy_bias(2, [0])
-        open_second(1)
-        copy_pre_sup(1, [0, 1])
         quantise_features(G - 2)
         edge(G - 2)
-        pre_sup(1, [2, 3])
         relu(G - 2)
         inverse_root_degrees(G - 2)
         normalise(G - 2)
+        open_codes(0)
         quantise_second(0)
-        spread_d(1)
-        bias_transposes(2, [1])
         product(0)
-        copy_pre_sup(1, [2, 3])
+        open_second(1)
+        pre_sup(1)
+        copy_pre_sup(1)
+        spread_d(1)
         scale_columns(1)
-        copy_bias(2, [1])
         quantise_features(G - 1)
-        add_bias(0)
         edge(G - 1)
         relu(G - 1)
         inverse_root_degrees(G - 1)
         normalise(G - 1)
+        add_bias(0)
+        open_second(2)
+        pre_sup(2)
+        copy_pre_sup(2)
+        open_codes(1)
         quantise_second(1)
-        tanh_and_store(0)
-        spread_d(2)
-        pre_sup(2, [0, 1])
         product(1)
-        for k in range(2, G + 1):
-            if k < G:
-                open_second(k)
-                scale_columns(k)
-                copy_pre_sup(k, [0])
-                pre_sup(k, [2])
-                if k > 2:
-                    copy_bias(k, [0])
-                    bias_transposes(k, [1])
-                copy_pre_sup(k, [1])
-                pre_sup(k, [3])
-                if k > 2:
-                    copy_bias(k, [1])
-                at(k + 1, spread_d)
-                if k + 1 < G:
-                    open_bias(k + 1)
-                    bias_transposes(k + 1, [0])
-                copy_pre_sup(k, [2])
-                if k + 1 < G:
-                    pre_sup(k + 1, [0])
-            add_bias(k - 1, [0])
-            tanh_and_store(k - 1, [0])
-            if k < G:
-                copy_pre_sup(k, [3])
-                if k + 1 < G:
-                    pre_sup(k + 1, [1])
-            for j in range(1, 4):
-                add_bias(k - 1, [j])
-                tanh_and_store(k - 1, [j])
-            if k < G:
-                quantise_second(k)
-                product(k)
+        tanh_and_store(0)
+        for k in range(2, G - 1):
+            spread_d(k)
+            scale_columns(k)
+            open_second(k + 1)
+            pre_sup(k + 1)
+            copy_pre_sup(k + 1)
+            if 3 < k:
+                open_bias(k)
+                bias_transposes(k, [0, 1])
+                copy_bias(k)
+            add_bias(k - 1)
+            tanh_and_store(k - 1)
+            open_codes(k)
+            quantise_second(k)
+            product(k)
+        k = G - 1
+        spread_d(k)
+        open_bias(k)
+        bias_transposes(k, [0, 1])
+        copy_bias(k)
+        open_codes(k)
+        quantise_second(k, N, 2 * N)
+        scale_columns(k, 0, HALF)
+        add_bias(k - 1, [0, 1])
+        quantise_second(k, 0, HALF)
+        product(k, [0, 2])
+        scale_columns(k, HALF, N)
+        add_bias(k - 1, [2, 3])
+        quantise_second(k, HALF, N)
+        product(k, [1, 3])
+        tanh_and_store(k - 1)
+        for j in (0, 2, 1, 3):
+            add_bias(k, [j])
+            tanh_and_store(k, [j])

@@ -367,15 +367,16 @@ def tile_graphlearner_pa_t_kernel(tc, feat, mask, W, b, out):
                 nc.scalar.activation(out=z[:], in_=z[:], func=ACT.Tanh)
                 nc.sync.dma_start(out=rows[u][:, :, HALF * h : HALF * h + HALF], in_=z[:])
 
+        pre_sup_at = {3: [0], 4: [1], 5: [2], 6: [3]}
         bias_at = {1: 0, 2: 1, 4: 2, 6: 3}
 
         def first_round(s):
             open_first(s)
             at(s + 1, diagonals)
-            if s < 3:
-                at(s + 2, gram)
+            at(s + 2, gram)
             if s >= 2:
                 quantise_features(s - 2)
+            if s >= 2:
                 edge(s - 2)
             at(s + 1, clamp_norms)
             at(s + 1, inverse_norms)
@@ -386,13 +387,11 @@ def tile_graphlearner_pa_t_kernel(tc, feat, mask, W, b, out):
                 relu(s - 2)
                 inverse_root_degrees(s - 2)
                 normalise(s - 2)
-            if s >= 3:
-                at(s + 2, gram)
-            if 3 <= s < 7:
+            if s in pre_sup_at:
                 if s == 3:
                     open_second(0)
-                pre_sup(0, [s - 3], early=True)
-                copy_pre_sup(0, [s - 3])
+                pre_sup(0, pre_sup_at[s], early=True)
+                copy_pre_sup(0, pre_sup_at[s])
             if s in bias_at:
                 open_bias(bias_at[s])
                 bias_transposes(bias_at[s], [0, 1], early=True)
@@ -428,9 +427,9 @@ def tile_graphlearner_pa_t_kernel(tc, feat, mask, W, b, out):
             load(5)
             load(6)
             load(7)
-            for s in range(1, 3):
+            for s in range(1, 7):
                 first_round(s)
-        for s in range(3, G):
+        for s in range(7, G):
             first_round(s)
         spread_d(0)
         scale_columns(0)

@@ -65,6 +65,7 @@ def tile_graphlearner_pa_t_kernel(tc, feat, mask, W, b, out):
         wscales = const.tile([P, D], U8, align_bytes=64)
         deg = const.tile([P, G, NT], F32)
         dv = const.tile([P, G, NT], F32)
+        dm = const.tile([P, G, NT], F32)
         rall = const.tile([P, (4 * G + 1) * N], F32)
         codes1 = []
         scales1 = []
@@ -254,20 +255,21 @@ def tile_graphlearner_pa_t_kernel(tc, feat, mask, W, b, out):
                 nc.gpsimd.tensor_scalar_add(out=dg2[:], in0=deg[:, g, :], scalar1=1.00000001)
                 nc.gpsimd.tensor_tensor(out=dv[:, g, :], in0=dg2[:], in1=neghalf[:], op=ALU.pow)
 
+        def masked_degrees(g):
+            nc.vector.tensor_tensor(
+                out=dm[:, g, :], in0=dv[:, g, :], in1=maskT[:, NT * g : NT * g + NT], op=ALU.mult
+            )
+
         def scale_rows(g):
             for t in range(4):
                 nc.gpsimd.tensor_scalar(
-                    out=r(g, t),
-                    in0=r(g, t),
-                    scalar1=dv[:, g, t : t + 1],
-                    scalar2=maskT[:, NT * g + t : NT * g + t + 1],
-                    op0=ALU.mult,
-                    op1=ALU.mult,
+                    out=r(g, t), in0=r(g, t), scalar1=dm[:, g, t : t + 1], scalar2=0.0, op0=ALU.mult, op1=ALU.add
                 )
 
         def normalise(g):
-            add_identity(g)
+            masked_degrees(g)
             scale_rows(g)
+            at(g + 1, add_identity)
 
         def spread_d(g):
             dbc = pone.tile([P, N], F32, tag="a")
@@ -373,9 +375,15 @@ def tile_graphlearner_pa_t_kernel(tc, feat, mask, W, b, out):
         def first_round(s):
             open_first(s)
             at(s + 1, diagonals)
+            if s == 6:
+                spread_d(0)
             at(s + 2, gram)
             if s >= 2:
                 quantise_features(s - 2)
+            if s == 4:
+                normalise(0)
+            if s == 6:
+                normalise(1)
             if s >= 2:
                 edge(s - 2)
             at(s + 1, clamp_norms)
@@ -386,7 +394,8 @@ def tile_graphlearner_pa_t_kernel(tc, feat, mask, W, b, out):
             if s >= 2:
                 relu(s - 2)
                 inverse_root_degrees(s - 2)
-                normalise(s - 2)
+                if s == 2:
+                    add_identity(0)
             if s in pre_sup_at:
                 if s == 3:
                     open_second(0)
@@ -427,19 +436,18 @@ def tile_graphlearner_pa_t_kernel(tc, feat, mask, W, b, out):
             load(5)
             load(6)
             load(7)
-            for s in range(1, 7):
+            for s in range(1, 8):
                 first_round(s)
-        for s in range(7, G):
+        for s in range(8, G):
             first_round(s)
-        spread_d(0)
         scale_columns(0)
         quantise_features(G - 2)
         edge(G - 2)
         relu(G - 2)
         inverse_root_degrees(G - 2)
-        normalise(G - 2)
         open_codes(0)
         quantise_second(0)
+        normalise(2)
         product(0)
         open_second(1)
         pre_sup(1)
@@ -449,14 +457,13 @@ def tile_graphlearner_pa_t_kernel(tc, feat, mask, W, b, out):
         quantise_features(G - 1)
         edge(G - 1)
         relu(G - 1)
-        inverse_root_degrees(G - 1)
-        normalise(G - 1)
         add_bias(0)
         open_second(2)
         pre_sup(2)
         copy_pre_sup(2)
         open_codes(1)
         quantise_second(1)
+        normalise(3)
         product(1)
         tanh_and_store(0)
         for k in range(2, G - 1):
@@ -473,6 +480,9 @@ def tile_graphlearner_pa_t_kernel(tc, feat, mask, W, b, out):
             tanh_and_store(k - 1)
             open_codes(k)
             quantise_second(k)
+            at(k + 2, normalise)
+            if k == 2:
+                inverse_root_degrees(G - 1)
             product(k)
         k = G - 1
         spread_d(k)

from contextlib import ExitStack

import concourse.mybir as mybir
from concourse.masks import make_identity

F32 = mybir.dt.float32
BF16 = mybir.dt.bfloat16
U32 = mybir.dt.uint32
U8 = mybir.dt.uint8
FP8X4 = mybir.dt.float8_e4m3fn_x4
ALU = mybir.AluOpType
ACT = mybir.ActivationFunctionType

P = 128
G = 8
N = 512
D = 512
NT = N // P
HALF = N // 2
FLOPS = 3 * 2 * G * N * N * D


def tile_graphlearner_pa_t_kernel(tc, feat, mask, W, b, out):
    nc = tc.nc

    def at(g, stage):
        if 0 <= g < G:
            stage(g)

    def quantise(codes, scales, grouped):
        nc.vector.quantize_mx(out=codes.bitcast(FP8X4), scales=scales, in_=grouped)

    def mx(dst, lcodes, lscales, rcodes, rscales):
        nc.tensor.matmul_mx(
            out=dst,
            lhsT=lcodes.bitcast(FP8X4),
            lhsT_scale=lscales,
            rhs=rcodes.bitcast(FP8X4),
            rhs_scale=rscales,
            start=True,
            stop=True,
        )

    with ExitStack() as ctx:
        const = ctx.enter_context(tc.tile_pool(name="const", bufs=1))
        feats = ctx.enter_context(tc.tile_pool(name="feats", bufs=5))
        work = ctx.enter_context(tc.tile_pool(name="work", bufs=2))
        small = ctx.enter_context(tc.tile_pool(name="small", bufs=4))
        fxpool = ctx.enter_context(tc.tile_pool(name="fxpool", bufs=3))
        bpool = ctx.enter_context(tc.tile_pool(name="bpool", bufs=4))
        zpool = ctx.enter_context(tc.tile_pool(name="zpool", bufs=8))
        ptr = ctx.enter_context(tc.psum_pool(name="ptr", bufs=2))
        pone = ctx.enter_context(tc.psum_pool(name="pone", bufs=1))
        pmm = ctx.enter_context(tc.psum_pool(name="pmm", bufs=4))

        ident_b = const.tile([P, P], BF16)
        ident_f = const.tile([P, P], F32)
        neghalf = const.tile([P, NT], F32)
        mrows = const.tile([P, P], BF16)
        first = const.tile([P, NT], F32)
        maskT = const.tile([P, G * NT], F32)
        dmf = const.tile([P, G * NT, P], F32)
        b_sb = const.tile([P, NT, D], BF16)
        wcodes = const.tile([P, D], U32, align_bytes=64)
        wscales = const.tile([P, D], U8, align_bytes=64)
        deg = const.tile([P, G, NT], F32)
        dv = const.tile([P, G, NT], F32)
        dm = const.tile([P, G, NT], F32)
        rall = const.tile([P, (4 * G + 1) * N], F32)
        codes1 = []
        scales1 = []
        f_sb = []
        T = []
        for g in range(G):
            codes1.append(const.tile([P, 2 * N], U32, align_bytes=64, name="c%d" % g))
            scales1.append(const.tile([P, 2 * N], U8, align_bytes=64, name="s%d" % g))
            f_sb.append(feats.tile([P, NT, D], BF16, tag="f", name="f%d" % g))
            T.append({})

        def r(g, t):
            return rall[:, 4 * N * g + N * t : 4 * N * g + N * t + N]

        wboth = fxpool.tile([P, 2 * N * 4], BF16, align_bytes=64, tag="fx")
        wraw = wboth[:, 0 : 4 * D].rearrange("p (t c) -> p t c", t=4)
        wg = wboth[:, 4 * D : 8 * D]

        def load(g):
            nc.sync.dma_start(out=f_sb[g][:], in_=feat[g].rearrange("(i p) d -> p i d", p=P))

        def constants_and_loads():
            make_identity(nc, ident_b[:])
            make_identity(nc, ident_f[:])
            nc.vector.memset(neghalf[:], -0.5)
            nc.vector.memset(mrows[:], 0.0)
            nc.scalar.activation(out=first[:], in_=neghalf[:], func=ACT.Abs_reciprocal_sqrt)
            nc.sync.dma_start(out=mrows[0 : G * NT, :], in_=mask.rearrange("g (i p) -> (g i) p", p=P))
            load(0)
            for u in range(2):
                nc.sync.dma_start(
                    out=wraw[:, 2 * u : 2 * u + 2, :],
                    in_=W[256 * u : 256 * u + 256, :].rearrange("(q e) c -> q e c", e=2),
                )
            load(1)
            nc.sync.dma_start(out=b_sb[:], in_=b.rearrange("(i p) e -> p i e", p=P))
            for g in range(2, 5):
                load(g)
            mT_ps = ptr.tile([P, P], BF16, tag="tr")
            nc.tensor.transpose(mT_ps[:], mrows[:], ident_b[:])
            nc.vector.tensor_copy(out=maskT[:], in_=mT_ps[:, 0 : G * NT])

        def masked_identity_vector(g):
            gs = slice(NT * g, NT * g + NT)
            nc.vector.tensor_tensor(
                out=dmf[:, gs, :],
                in0=ident_f[:].unsqueeze(1).to_broadcast([P, NT, P]),
                in1=maskT[:, gs].unsqueeze(2).to_broadcast([P, NT, P]),
                op=ALU.mult,
            )

        def masked_identity_gpsimd(g):
            for i in range(NT):
                nc.gpsimd.tensor_scalar(
                    out=dmf[:, NT * g + i, :],
                    in0=ident_f[:],
                    scalar1=maskT[:, NT * g + i : NT * g + i + 1],
                    scalar2=0.0,
                    op0=ALU.mult,
                    op1=ALU.add,
                )

        def copy_w():
            for u in range(2):
                for e in range(2):
                    nc.gpsimd.tensor_scalar(
                        out=wg.rearrange("p (u e q t) -> p u e q t", u=2, e=2, t=4)[:, u, e],
                        in0=wraw.rearrange("p t (u q e) -> p u e q t", u=2, e=2)[:, u, e],
                        scalar1=1.0,
                        scalar2=0.0,
                        op0=ALU.mult,
                        op1=ALU.add,
                    )

        def gram(g):
            gr = pone.tile([P, 4, P], F32, tag="ab"[g % 2])
            T[g]["gr"] = gr
            columns = f_sb[g][:].rearrange("p i (u q e) -> p i u e q", u=2, e=2)
            for u in range(2):
                for e in range(2):
                    for i in range(NT):
                        block = columns[:, i, u, e, :]
                        nc.tensor.matmul(gr[:, 2 * u + e, :], lhsT=block, rhs=block, start=(i == 0), stop=(i == NT - 1))

        def diagonals(g):
            ss = small.tile([P, 4], F32)
            T[g]["ss"] = ss
            for t in range(4):
                junk = small.tile([P, P], F32)
                nc.vector.scalar_tensor_tensor(
                    out=junk[:],
                    in0=T[g]["gr"][:, t, :],
                    scalar=1.0,
                    in1=ident_f[:],
                    op0=ALU.mult,
                    op1=ALU.mult,
                    accum_out=ss[:, t : t + 1],
                )

        def clamp_norms(g):
            ssm = small.tile([P, 4], F32)
            T[g]["ssm"] = ssm
            nc.vector.tensor_scalar_max(out=ssm[:], in0=T[g]["ss"][:], scalar1=1e-24)

        def inverse_norms(g):
            rn = small.tile([P, 4], F32)
            T[g]["rn"] = rn
            nc.scalar.activation(out=rn[:], in_=T[g]["ssm"][:], func=ACT.Abs_reciprocal_sqrt)

        def masked_transposes(g, halves=range(2)):
            for h in halves:
                if g == 1:
                    ft = pmm.tile([P, 2, HALF], F32, tag="mm")
                else:
                    ft = ptr.tile([P, 2, HALF], F32, tag="tr")
                T[g]["ft" + str(h)] = ft
                for u in range(2):
                    for ii in range(2):
                        i = 2 * h + ii
                        nc.tensor.transpose(
                            ft[:, u, P * ii : P * ii + P],
                            f_sb[g][:, i, :].bitcast(F32)[:, P * u : P * u + P],
                            dmf[:, NT * g + i, :],
                        )

        def copy_features(g, halves=range(2)):
            fg32 = T[g]["fx"][:, 0 : 4 * N].bitcast(F32).rearrange("p (n u) -> p n u", u=2)
            for h in halves:
                nc.scalar.copy(
                    out=fg32[:, HALF * h : HALF * h + HALF, :], in_=T[g]["ft" + str(h)][:].rearrange("p u n -> p n u")
                )

        def open_first(g):
            fx = fxpool.tile([P, 2 * N * 4], BF16, align_bytes=64, tag="fx")
            T[g]["fx"] = fx

        def normed_features(g, halves=range(2)):
            xg4 = T[g]["fx"][:, 4 * N : 8 * N].rearrange("p (n u e) -> p n u e", u=2, e=2)
            for h in halves:
                nc.vector.tensor_tensor(
                    out=xg4[:, HALF * h : HALF * h + HALF, :, :],
                    in0=T[g]["ft" + str(h)][:]
                    .rearrange("p u n -> p (u n)")
                    .bitcast(BF16)
                    .rearrange("p (u n e) -> p n u e", u=2, e=2),
                    in1=T[g]["rn"][:].rearrange("p (u e) -> p u e", e=2).unsqueeze(1).to_broadcast([P, HALF, 2, 2]),
                    op=ALU.mult,
                )

        def normed_features_gpsimd(g):
            for c in range(4):
                cols = slice(N * c, N * c + N)
                nc.gpsimd.tensor_tensor(
                    out=T[g]["fx"][:, 4 * N : 8 * N][:, cols].rearrange("p (n t) -> p n t", t=4),
                    in0=T[g]["fx"][:, cols].rearrange("p (n t) -> p n t", t=4),
                    in1=T[g]["rn"][:].unsqueeze(1).to_broadcast([P, P, 4]),
                    op=ALU.mult,
                )

        def quantise_features(g):
            quantise(codes1[g][:], scales1[g][:], T[g]["fx"][:])

        def edge(g):
            xc = codes1[g][:, N : 2 * N]
            xs = scales1[g][:, N : 2 * N]
            for t in range(4):
                et = pmm.tile([P, N], F32, tag="mm")
                T[g]["et" + str(t)] = et
                cols = slice(P * t, P * t + P)
                mx(et[:], xc[:, cols], xs[:, cols], xc, xs)

        def relu(g, planes=range(4)):
            for t in planes:
                nc.scalar.activation(out=r(g, t), in_=T[g]["et" + str(t)][:], func=ACT.Relu, accum_out=deg[:, g, t : t + 1])

        def add_identity(g):
            rdiag = rall[:, 4 * N * g : 4 * N * g + 5 * N].rearrange("p (t s) -> p t s", s=N + P)[:, :, 0:P]
            nc.gpsimd.tensor_tensor(
                out=rdiag, in0=rdiag, in1=ident_f[:].unsqueeze(1).to_broadcast([P, 4, P]), op=ALU.add
            )

        def inverse_root_degrees(g):
            if g < G - 1:
                nc.scalar.activation(out=dv[:, g, :], in_=deg[:, g, :], func=ACT.Abs_reciprocal_sqrt, bias=1.00000001)
            else:
                dg2 = small.tile([P, NT], F32)
                nc.gpsimd.tensor_scalar_add(out=dg2[:], in0=deg[:, g, :], scalar1=1.00000001)
                nc.gpsimd.tensor_tensor(out=dv[:, g, :], in0=dg2[:], in1=neghalf[:], op=ALU.pow)

        def masked_degrees(g):
            nc.vector.tensor_tensor(
                out=dm[:, g, :], in0=dv[:, g, :], in1=maskT[:, NT * g : NT * g + NT], op=ALU.mult
            )

        def scale_rows(g):
            for t in range(4):
                nc.gpsimd.tensor_scalar(
                    out=r(g, t), in0=r(g, t), scalar1=dm[:, g, t : t + 1], scalar2=0.0, op0=ALU.mult, op1=ALU.add
                )

        def normalise(g):
            masked_degrees(g)
            scale_rows(g)
            at(g + 1, add_identity)

        def spread_d(g):
            dbc = pone.tile([P, N], F32, tag="a")
            T[g]["dbc"] = dbc
            for i in range(NT):
                nc.tensor.transpose(dbc[:, P * i : P * i + P], dv[:, g, i : i + 1].to_broadcast([P, P]), ident_f[:])

        def pre_sup(g, blocks=range(4), early=False):
            for j in blocks:
                if early:
                    pj = pmm.tile([P, 4, P], F32, tag="mm")
                else:
                    pj = ptr.tile([P, 4, P], F32, tag="tr")
                T[g]["pj" + str(j)] = pj
                cols = slice(P * j, P * j + P)
                for t in range(4):
                    rows = slice(P * t, P * t + P)
                    mx(pj[:, t, :], codes1[g][:, rows], scales1[g][:, rows], wcodes[:, cols], wscales[:, cols])

        def copy_pre_sup(g, blocks=range(4)):
            psg3 = T[g]["ap"][:, 4 * N : 8 * N].rearrange("p (e t) -> p e t", t=4)
            for j in blocks:
                nc.scalar.copy(out=psg3[:, P * j : P * j + P, :], in_=T[g]["pj" + str(j)][:].rearrange("p t e -> p e t"))

        def open_second(g):
            ap = work.tile([P, 2 * N * 4], BF16, align_bytes=64)
            T[g]["ap"] = ap

        def scale_columns(g, lo=0, hi=N):
            n4 = (hi - lo) // 4
            nc.vector.tensor_tensor(
                out=T[g]["ap"][:, 4 * lo : 4 * hi].rearrange("p (c i t) -> p c t i", i=4, t=4),
                in0=rall[:, 4 * N * g : 4 * N * g + 4 * N]
                .rearrange("p (t n) -> p t n", t=4)[:, :, lo:hi]
                .rearrange("p t (c i) -> p c t i", i=4),
                in1=T[g]["dbc"][:, lo:hi].rearrange("p (c i) -> p c i", i=4).unsqueeze(2).to_broadcast([P, n4, 4, 4]),
                op=ALU.mult,
            )

        def open_codes(g):
            c2 = work.tile([P, 2 * N], U32, align_bytes=64)
            s2 = work.tile([P, 2 * N], U8, align_bytes=64)
            T[g]["c2"] = c2
            T[g]["s2"] = s2

        def quantise_second(g, lo=0, hi=2 * N):
            quantise(T[g]["c2"][:, lo:hi], T[g]["s2"][:, lo:hi], T[g]["ap"][:, 4 * lo : 4 * hi])

        def bias_transposes(g, words, early=False):
            for u in words:
                if early:
                    bt = pmm.tile([P, N], F32, tag="mm")
                else:
                    bt = pone.tile([P, N], F32, tag="b")
                T[g]["bt" + str(u)] = bt
                for i in range(NT):
                    nc.tensor.transpose(
                        bt[:, P * i : P * i + P],
                        b_sb[:, i, :].bitcast(F32)[:, P * u : P * u + P],
                        dmf[:, NT * g + i, :],
                    )

        def open_bias(g):
            bm = bpool.tile([P, 2, 2 * N], BF16)
            T[g]["bm"] = bm

        def copy_bias(g, words=range(2)):
            bm = T[g]["bm"]
            for u in words:
                nc.scalar.copy(out=bm[:, u, :].bitcast(F32), in_=T[g]["bt" + str(u)][:])

        def product(g, banks=range(4)):
            c2 = T[g]["c2"]
            s2 = T[g]["s2"]
            for j in banks:
                u, h = j // 2, j % 2
                oj = pmm.tile([P, 2, HALF], F32, tag="mm")
                T[g]["oj" + str(j)] = oj
                cols = slice(HALF * h, HALF * h + HALF)
                for e in range(2):
                    rows = slice(N + P * (2 * u + e), N + P * (2 * u + e) + P)
                    mx(oj[:, e, :], c2[:, rows], s2[:, rows], c2[:, cols], s2[:, cols])

        def add_bias(g, banks=range(4)):
            for j in banks:
                u, h = j // 2, j % 2
                z = zpool.tile([P, 2, HALF], F32)
                T[g]["z" + str(j)] = z
                bias = T[g]["bm"][:, u, :].rearrange("p (n e) -> p e n", e=2)[:, :, HALF * h : HALF * h + HALF]
                nc.vector.tensor_tensor(out=z[:], in0=T[g]["oj" + str(j)][:], in1=bias, op=ALU.add)

        def tanh_and_store(g, banks=range(4)):
            rows = out[g].rearrange("(u q e) n -> u q e n", u=2, e=2)
            for j in banks:
                u, h = j // 2, j % 2
                z = T[g]["z" + str(j)]
                nc.scalar.activation(out=z[:], in_=z[:], func=ACT.Tanh)
                nc.sync.dma_start(out=rows[u][:, :, HALF * h : HALF * h + HALF], in_=z[:])

        pre_sup_at = {3: [0], 4: [1], 5: [2], 6: [3]}
        bias_at = {1: 0, 2: 1, 4: 2, 6: 3}

        def first_round(s):
            open_first(s)
            at(s + 1, diagonals)
            if s == 6:
                spread_d(0)
            at(s + 2, gram)
            if s >= 2:
                quantise_features(s - 2)
            if s == 4:
                normalise(0)
            if s == 6:
                normalise(1)
            if s >= 2:
                edge(s - 2)
            at(s + 1, clamp_norms)
            at(s + 1, inverse_norms)
            normed_features(s)
            copy_features(s)
            at(s + 1, masked_transposes)
            if s >= 2:
                relu(s - 2)
                inverse_root_degrees(s - 2)
                if s == 2:
                    add_identity(0)
            if s in pre_sup_at:
                if s == 3:
                    open_second(0)
                pre_sup(0, pre_sup_at[s], early=True)
                copy_pre_sup(0, pre_sup_at[s])
            if s in bias_at:
                open_bias(bias_at[s])
                bias_transposes(bias_at[s], [0, 1], early=True)
                copy_bias(bias_at[s])

        ctx.enter_context(
            tc.manual_schedule(engines={mybir.EngineType.DVE, mybir.EngineType.Pool, mybir.EngineType.SP})
        )
        with tc.manual_schedule(engines={mybir.EngineType.PE}):
            with tc.manual_schedule(engines={mybir.EngineType.Activation}):
                constants_and_loads()
                for g in range(3):
                    masked_identity_vector(g)
                masked_identity_gpsimd(3)
                copy_w()
                for g in range(4, G):
                    masked_identity_gpsimd(g)
                gram(0)
                masked_transposes(0)
                gram(1)
                masked_transposes(1)
                diagonals(0)
                clamp_norms(0)
                inverse_norms(0)
                open_first(0)
                normed_features(0)
                copy_features(0)
                diagonals(1)
                clamp_norms(1)
                inverse_norms(1)
            gram(2)
            quantise(wcodes[:], wscales[:], wg[:])
            load(5)
            load(6)
            load(7)
            for s in range(1, 8):
                first_round(s)
        for s in range(8, G):
            first_round(s)
        scale_columns(0)
        quantise_features(G - 2)
        edge(G - 2)
        relu(G - 2)
        inverse_root_degrees(G - 2)
        open_codes(0)
        quantise_second(0)
        normalise(2)
        product(0)
        open_second(1)
        pre_sup(1)
        copy_pre_sup(1)
        spread_d(1)
        scale_columns(1)
        quantise_features(G - 1)
        edge(G - 1)
        relu(G - 1)
        add_bias(0)
        open_second(2)
        pre_sup(2)
        copy_pre_sup(2)
        open_codes(1)
        quantise_second(1)
        normalise(3)
        product(1)
        tanh_and_store(0)
        for k in range(2, G - 1):
            spread_d(k)
            scale_columns(k)
            open_second(k + 1)
            pre_sup(k + 1)
            copy_pre_sup(k + 1)
            if 3 < k:
                open_bias(k)
                bias_transposes(k, [0, 1])
                copy_bias(k)
            add_bias(k - 1)
            tanh_and_store(k - 1)
            open_codes(k)
            quantise_second(k)
            at(k + 2, normalise)
            if k == 2:
                inverse_root_degrees(G - 1)
            product(k)
        k = G - 1
        spread_d(k)
        open_bias(k)
        bias_transposes(k, [0, 1])
        copy_bias(k)
        open_codes(k)
        quantise_second(k, N, 2 * N)
        scale_columns(k, 0, HALF)
        add_bias(k - 1, [0, 1])
        quantise_second(k, 0, HALF)
        product(k, [0, 2])
        scale_columns(k, HALF, N)
        add_bias(k - 1, [2, 3])
        quantise_second(k, HALF, N)
        product(k, [1, 3])
        tanh_and_store(k - 1)
        for j in (0, 2, 1, 3):
            add_bias(k, [j])
            tanh_and_store(k, [j])
